import numpy as np
import ml_dtypes


def mxq(x, axis, fmt="e4m3"):
    dtype, down = {"e4m3": (ml_dtypes.float8_e4m3fn, 7), "e5m2": (ml_dtypes.float8_e5m2, 14)}[fmt]
    v = np.moveaxis(np.asarray(x, np.float32).astype(ml_dtypes.bfloat16).astype(np.float64), axis, -1)
    blocks = v.reshape(v.shape[:-1] + (-1, 32))
    amax = np.abs(blocks).max(-1, keepdims=True)
    byte = np.maximum(np.where(amax > 0, np.frexp(amax)[1] - 1 + 127, 0) - down, 1)
    scale = np.exp2(byte - 127.0)
    codes = (blocks / scale).astype(np.float32).astype(dtype).astype(np.float64)
    return np.moveaxis((codes * scale).reshape(v.shape), -1, axis)


WIDE = False


def mx_kscale(k):
    if not WIDE:
        return np.ones(k)
    levels = np.array([10, -10, 5, -5, 0])
    a = np.random.permutation(np.resize(levels, k // 512 * 4)).reshape(k // 512, 4)
    idx = np.arange(k)
    return np.exp2(a[idx // 512, idx % 128 // 32])


BF16 = ml_dtypes.bfloat16


def bf(x):
    return np.asarray(x, np.float32).astype(BF16)


def f64(x):
    return np.asarray(x).astype(np.float64)


E2M1 = np.array([0.0, 0.5, 1.0, 1.5, 2.0, 3.0, 4.0, 6.0, -0.0, -0.5, -1.0, -1.5, -2.0, -3.0, -4.0, -6.0])


def pack_weight(w, fmt):
    k, n = w.shape
    w = f64(bf(w)).reshape(k // 32, 32, n)
    amax = np.abs(w).max(1)
    if fmt == "e4m3":
        byte = np.frexp(amax)[1] - 1 + 127 - 7
    else:
        mant, ex = np.frexp(amax / 6.0)
        byte = np.where(mant > 0.5, ex, ex - 1) + 127
    byte = np.clip(np.where(amax > 0, byte, 1), 1, 254)
    scaled = (w * np.exp2(127.0 - byte)[:, None, :]).reshape(k, n).astype(np.float32)
    by_word = np.ascontiguousarray(scaled.reshape(k // 512, 128, 4, n).transpose(0, 1, 3, 2))
    if fmt == "e4m3":
        words = by_word.astype(ml_dtypes.float8_e4m3fn).view(np.uint8)
    else:
        c = by_word.astype(ml_dtypes.float4_e2m1fn).view(np.uint8) & 0xF
        words = c[..., 0::2] | (c[..., 1::2] << 4)
    return np.ascontiguousarray(words), np.ascontiguousarray(byte.astype(np.uint8).reshape(k // 512, 16, n))


def unpack_weight(words, scales, fmt):
    g, p, n, _ = words.shape
    if fmt == "e4m3":
        vals = np.ascontiguousarray(words).view(ml_dtypes.float8_e4m3fn).astype(np.float64)
    else:
        nib = np.empty((g, p, n, 4), np.uint8)
        nib[..., 0::2] = words & 0xF
        nib[..., 1::2] = words >> 4
        vals = E2M1[nib]
    vals = vals * np.repeat(np.exp2(scales.astype(np.float64) - 127.0), 8, axis=1)[..., None]
    return vals.transpose(0, 1, 3, 2).reshape(g * 512, n)


B, S, H, NH, NKV, HD = 4, 2048, 1024, 2, 1, 128
EPS = 1e-6
FMT = "e4m3"


def rms_norm(x, w):
    var = np.mean(x * x, axis=-1, keepdims=True)
    return x * (1.0 / np.sqrt(var + EPS)) * w


def rotate_half(x):
    x1, x2 = np.split(x, 2, axis=-1)
    return np.concatenate([-x2, x1], axis=-1)


def setup_inputs():
    s = mx_kscale(H)
    inv_freq = 1.0 / (10000.0 ** (np.arange(0, HD, 2) / HD))
    freqs = np.arange(S)[:, None] * inv_freq[None, :]
    emb = np.concatenate([freqs, freqs], axis=-1)
    hidden_states = bf(np.random.standard_normal((B, S, H)) * s)
    wq = np.random.standard_normal((NH * HD, H)) / np.sqrt(H) / s[None, :]
    wk = np.random.standard_normal((NKV * HD, H)) / np.sqrt(H) / s[None, :]
    wq_words, wq_scales = pack_weight(np.ascontiguousarray(wq.T), FMT)
    wk_words, wk_scales = pack_weight(np.ascontiguousarray(wk.T), FMT)
    return {"hidden_states": hidden_states,
            "cos": bf(np.cos(emb)),
            "sin": bf(np.sin(emb)),
            "wq_words": wq_words,
            "wq_scales": wq_scales,
            "wk_words": wk_words,
            "wk_scales": wk_scales,
            "q_norm_w": bf(1.0 + 0.1 * np.random.standard_normal(HD)),
            "k_norm_w": bf(1.0 + 0.1 * np.random.standard_normal(HD)),
            "ssmax_scale": bf((1.0 + 0.2 * np.random.standard_normal((1, NH, 1, 1))) / np.log(S))}


def reference(hidden_states, cos, sin, wq_words, wq_scales, wk_words, wk_scales, q_norm_w, k_norm_w, ssmax_scale):
    xq = mxq(f64(hidden_states), 2, "e4m3")
    q = (xq @ unpack_weight(wq_words, wq_scales, FMT)).reshape(B, S, NH, HD)
    k = (xq @ unpack_weight(wk_words, wk_scales, FMT)).reshape(B, S, NKV, HD)
    q = rms_norm(q, f64(q_norm_w)).transpose(0, 2, 1, 3)
    k = rms_norm(k, f64(k_norm_w)).transpose(0, 2, 1, 3)
    c = f64(cos)[None, None]
    sn = f64(sin)[None, None]
    q = q * c + rotate_half(q) * sn
    k = k * c + rotate_half(k) * sn
    q = q * (f64(ssmax_scale) * np.log(S))
    return q, k

@@ -1,0 +1,342 @@
+import math
+from contextlib import ExitStack
+
+import concourse.mybir as mybir
+from concourse.masks import make_identity
+
+F32 = mybir.dt.float32
+BF16 = mybir.dt.bfloat16
+I32 = mybir.dt.int32
+U32 = mybir.dt.uint32
+U8 = mybir.dt.uint8
+FP8X4 = mybir.dt.float8_e4m3fn_x4
+ALU = mybir.AluOpType
+ACT = mybir.ActivationFunctionType
+
+P = 128
+BATCH = 4
+SEQ = 2048
+HIDDEN = 1024
+HEAD_DIM = 128
+HALF = HEAD_DIM // 2
+Q_HEADS = 2
+HEADS = Q_HEADS + 1
+Q_COLS = Q_HEADS * HEAD_DIM
+OUT_COLS = HEADS * HEAD_DIM
+EPS = 1e-6
+
+K_PASS = 512
+PASSES = HIDDEN // K_PASS
+WORDS_PER_PASS = K_PASS // 2
+
+POS_PER_PART = SEQ // P
+CHUNK = 4
+CHUNKS = POS_PER_PART // CHUNK
+GROUPS = CHUNKS * BATCH
+UNIT = 2
+UNITS_PER_GROUP = CHUNK // UNIT
+UNITS = GROUPS * UNITS_PER_GROUP
+X_BUFS = 4
+
+FLOPS = 2 * BATCH * SEQ * HIDDEN * OUT_COLS
+
+
+def tile_biboattention_pa_t_kernel(
+    tc,
+    hidden_states,
+    cos,
+    sin,
+    wq_words,
+    wq_scales,
+    wk_words,
+    wk_scales,
+    q_norm_w,
+    k_norm_w,
+    ssmax_scale,
+    out_0,
+    out_1,
+):
+    nc = tc.nc
+
+    x_view = hidden_states.rearrange("b (p j) k -> b p j k", j=POS_PER_PART)
+    cos_view = cos.rearrange("(p j) d -> p j d", j=POS_PER_PART)
+    sin_view = sin.rearrange("(p j) d -> p j d", j=POS_PER_PART)
+    q_view = out_0.rearrange("b h (p j) d -> b p h j d", j=POS_PER_PART)
+    k_view = out_1.rearrange("b h (p j) d -> b h p j d", j=POS_PER_PART)
+
+    with ExitStack() as ctx:
+        keep = ctx.enter_context(tc.tile_pool(name="keep", bufs=1))
+        x_pool = ctx.enter_context(tc.tile_pool(name="x", bufs=X_BUFS))
+        mx_pool = ctx.enter_context(tc.tile_pool(name="mx", bufs=3))
+        row_pool = ctx.enter_context(tc.tile_pool(name="row", bufs=3))
+        work = ctx.enter_context(tc.tile_pool(name="work", bufs=3))
+        res_pool = ctx.enter_context(tc.tile_pool(name="res", bufs=3))
+        psum_t = ctx.enter_context(tc.psum_pool(name="psum_t", bufs=2 * UNIT))
+        psum_o = ctx.enter_context(tc.psum_pool(name="psum_o", bufs=2 * UNIT))
+        ctx.enter_context(tc.manual_schedule())
+
+        x_tiles = {}
+        xt_tiles = {}
+        grouped_tiles = {}
+        code_tiles = {}
+        acc_tiles = {}
+        rms_tiles = {}
+        scale_tiles = {}
+        term_tiles = {}
+        res_tiles = {}
+
+        def load_x(group):
+            c, b = divmod(group, BATCH)
+            x_sb = x_pool.tile([P, CHUNK, HIDDEN], BF16, name="x_sb")
+            nc.sync.dma_start(out=x_sb[:], in_=x_view[b][:, c * CHUNK : (c + 1) * CHUNK, :])
+            x_tiles[group] = x_sb
+
+        load_x(0)
+
+        w_codes = keep.tile([P, PASSES, OUT_COLS], U32, name="w_codes", align_bytes=64)
+        nc.sync.dma_start(
+            out=w_codes[:, :, 0:Q_COLS].bitcast(I32),
+            in_=wq_words.rearrange("g p n t -> p g (n t)").bitcast(I32),
+        )
+        nc.sync.dma_start(
+            out=w_codes[:, :, Q_COLS:OUT_COLS].bitcast(I32),
+            in_=wk_words.rearrange("g p n t -> p g (n t)").bitcast(I32),
+        )
+        w_scales = keep.tile([P, PASSES, OUT_COLS], U8, name="w_scales", align_bytes=64)
+        nc.vector.memset(w_scales[:].bitcast(I32), 0)
+        for quad in range(4):
+            rows = slice(4 * quad, 4 * quad + 4)
+            parts = slice(32 * quad, 32 * quad + 4)
+            nc.sync.dma_start(
+                out=w_scales[parts, :, 0:Q_COLS].bitcast(I32),
+                in_=wq_scales[:, rows, :].rearrange("g r n -> r g n").bitcast(I32),
+            )
+            nc.sync.dma_start(
+                out=w_scales[parts, :, Q_COLS:OUT_COLS].bitcast(I32),
+                in_=wk_scales[:, rows, :].rearrange("g r n -> r g n").bitcast(I32),
+            )
+
+        ident = keep.tile([P, P], F32, name="ident")
+        make_identity(nc, ident[:])
+
+        eps_col = keep.tile([P, 1], F32, name="eps_col")
+        nc.vector.memset(eps_col[:], EPS)
+
+        gain_bf = keep.tile([P, Q_HEADS], BF16, name="gain_bf")
+        nc.scalar.dma_start(
+            out=gain_bf[:], in_=ssmax_scale.rearrange("a h b c -> (a h b c)").partition_broadcast(P)
+        )
+        gain = keep.tile([P, HEADS], F32, name="gain")
+        nc.vector.memset(gain[:], 1.0)
+        nc.vector.tensor_scalar_mul(out=gain[:, 0:Q_HEADS], in0=gain_bf[:], scalar1=math.log(SEQ))
+
+        w_own = []
+        w_partner = []
+        for name, vec in (("q", q_norm_w), ("k", k_norm_w)):
+            own = keep.tile([P, HEAD_DIM], BF16, name="w_own_" + name)
+            nc.scalar.dma_start(out=own[:], in_=vec.partition_broadcast(P))
+            partner = keep.tile([P, HEAD_DIM], BF16, name="w_partner_" + name)
+            nc.vector.tensor_scalar_mul(out=partner[:, 0:HALF], in0=own[:, HALF:HEAD_DIM], scalar1=-1.0)
+            nc.vector.tensor_copy(out=partner[:, HALF:HEAD_DIM], in_=own[:, 0:HALF])
+            w_own.append(own)
+            w_partner.append(partner)
+
+        cos_sb = keep.tile([P, POS_PER_PART, HEAD_DIM], BF16, name="cos_sb")
+        sin_sb = keep.tile([P, POS_PER_PART, HEAD_DIM], BF16, name="sin_sb")
+        cos_w = []
+        sin_w = []
+        for name in ("q", "k"):
+            cos_tab = keep.tile([P, POS_PER_PART, HEAD_DIM], F32, name="cos_w_" + name)
+            sin_tab = keep.tile([P, POS_PER_PART, HEAD_DIM], F32, name="sin_w_" + name)
+            cos_w.append(cos_tab)
+            sin_w.append(sin_tab)
+
+        def load_cos_sin(c):
+            js = slice(c * CHUNK, (c + 1) * CHUNK)
+            nc.scalar.dma_start(out=cos_sb[:, js, :], in_=cos_view[:, js, :])
+            nc.scalar.dma_start(out=sin_sb[:, js, :], in_=sin_view[:, js, :])
+
+        def build_tables(c):
+            js = slice(c * CHUNK, (c + 1) * CHUNK)
+            for kind in range(2):
+                nc.gpsimd.tensor_tensor(
+                    out=cos_w[kind][:, js, :],
+                    in0=cos_sb[:, js, :],
+                    in1=w_own[kind][:].unsqueeze(1).to_broadcast([P, CHUNK, HEAD_DIM]),
+                    op=ALU.mult,
+                )
+                nc.gpsimd.tensor_tensor(
+                    out=sin_w[kind][:, js, :],
+                    in0=sin_sb[:, js, :],
+                    in1=w_partner[kind][:].unsqueeze(1).to_broadcast([P, CHUNK, HEAD_DIM]),
+                    op=ALU.mult,
+                )
+
+        load_cos_sin(0)
+        build_tables(0)
+        load_x(1)
+        load_cos_sin(1)
+        for group in range(2, X_BUFS):
+            load_x(group)
+
+        def transpose_unit(n):
+            group, part = divmod(n, UNITS_PER_GROUP)
+            for t in range(UNIT):
+                words = x_tiles[group][:, part * UNIT + t, :].bitcast(F32)
+                xt = psum_t.tile([P, PASSES * 2, P], F32, name="xt")
+                for g in range(PASSES):
+                    for u in range(2):
+                        first = WORDS_PER_PASS * g + u
+                        nc.tensor.transpose(
+                            xt[:, 2 * g + u, :], words[:, first : WORDS_PER_PASS * (g + 1) : 2], ident[:]
+                        )
+                xt_tiles[(n, t)] = xt
+
+        def regroup_unit(n):
+            grouped = mx_pool.tile([P, UNIT, HIDDEN], BF16, name="grouped", align_bytes=64)
+            for t in range(UNIT):
+                nc.scalar.copy(
+                    out=grouped[:, t, :].bitcast(F32).rearrange("p (g r u) -> p g r u", g=PASSES, u=2),
+                    in_=xt_tiles[(n, t)][:].rearrange("p (g u) r -> p g r u", u=2),
+                )
+            grouped_tiles[n] = grouped
+
+        def quantise_unit(n):
+            x_codes = mx_pool.tile([P, UNIT * PASSES * P], U32, name="x_codes", align_bytes=64)
+            x_scales = mx_pool.tile([P, UNIT * PASSES * P], U8, name="x_scales", align_bytes=64)
+            nc.vector.quantize_mx(
+                out=x_codes[:].bitcast(FP8X4),
+                scales=x_scales[:],
+                in_=grouped_tiles[n][:].rearrange("p t c -> p (t c)"),
+            )
+            code_tiles[n] = (x_codes, x_scales)
+
+        def project_unit(n):
+            x_codes, x_scales = code_tiles[n]
+            for t in range(UNIT):
+                acc = psum_o.tile([P, OUT_COLS], F32, name="acc")
+                for lo, hi in ((0, Q_COLS), (Q_COLS, OUT_COLS)):
+                    for g in range(PASSES):
+                        tokens = slice((t * PASSES + g) * P, (t * PASSES + g + 1) * P)
+                        nc.tensor.matmul_mx(
+                            out=acc[:, lo:hi],
+                            lhsT=x_codes[:, tokens].bitcast(FP8X4),
+                            lhsT_scale=x_scales[:, tokens],
+                            rhs=w_codes[:, g, lo:hi].bitcast(FP8X4),
+                            rhs_scale=w_scales[:, g, lo:hi],
+                            start=(g == 0),
+                            stop=(g == PASSES - 1),
+                        )
+                acc_tiles[(n, t)] = acc
+
+        def root_mean_square_unit(n):
+            sumsq = row_pool.tile([P, HEADS, UNIT], F32, name="sumsq")
+            squares = work.tile([P, HEADS, UNIT, HEAD_DIM], BF16, name="squares")
+            for t in range(UNIT):
+                for h in range(HEADS):
+                    nc.scalar.activation(
+                        out=squares[:, h, t, :],
+                        in_=acc_tiles[(n, t)][:, h * HEAD_DIM : (h + 1) * HEAD_DIM],
+                        func=ACT.Square,
+                        accum_out=sumsq[:, h, t : t + 1],
+                    )
+            rms = row_pool.tile([P, HEADS, UNIT], F32, name="rms")
+            nc.scalar.activation(
+                out=rms[:], in_=sumsq[:], func=ACT.Sqrt, scale=1.0 / HEAD_DIM, bias=eps_col[:, 0:1]
+            )
+            rms_tiles[n] = rms
+
+        def row_scale_unit(n):
+            inv_rms = row_pool.tile([P, HEADS, UNIT], F32, name="inv_rms")
+            nc.vector.reciprocal(out=inv_rms[:], in_=rms_tiles[n][:])
+            row_scale = row_pool.tile([P, HEADS, UNIT], F32, name="row_scale")
+            nc.vector.tensor_tensor(
+                out=row_scale[:],
+                in0=inv_rms[:],
+                in1=gain[:].unsqueeze(2).to_broadcast([P, HEADS, UNIT]),
+                op=ALU.mult,
+            )
+            scale_tiles[n] = row_scale
+
+        def rotary_terms_unit(n):
+            group, part = divmod(n, UNITS_PER_GROUP)
+            c = group // BATCH
+            row_scale = scale_tiles[n]
+            own_term = work.tile([P, HEADS, UNIT, HEAD_DIM], F32, name="own_term")
+            partner_term = work.tile([P, HEADS, UNIT, HEAD_DIM], F32, name="partner_term")
+            for t in range(UNIT):
+                j = c * CHUNK + part * UNIT + t
+                acc = acc_tiles[(n, t)]
+                for h in range(HEADS):
+                    kind = 0 if h < Q_HEADS else 1
+                    base = h * HEAD_DIM
+                    factor = row_scale[:, h, t : t + 1]
+                    nc.vector.scalar_tensor_tensor(
+                        out=own_term[:, h, t, :],
+                        in0=acc[:, base : base + HEAD_DIM],
+                        scalar=factor,
+                        in1=cos_w[kind][:, j, :],
+                        op0=ALU.mult,
+                        op1=ALU.mult,
+                    )
+                    nc.vector.scalar_tensor_tensor(
+                        out=partner_term[:, h, t, 0:HALF],
+                        in0=acc[:, base + HALF : base + HEAD_DIM],
+                        scalar=factor,
+                        in1=sin_w[kind][:, j, 0:HALF],
+                        op0=ALU.mult,
+                        op1=ALU.mult,
+                    )
+                    nc.vector.scalar_tensor_tensor(
+                        out=partner_term[:, h, t, HALF:HEAD_DIM],
+                        in0=acc[:, base : base + HALF],
+                        scalar=factor,
+                        in1=sin_w[kind][:, j, HALF:HEAD_DIM],
+                        op0=ALU.mult,
+                        op1=ALU.mult,
+                    )
+            term_tiles[n] = (own_term, partner_term)
+
+        def add_unit(n):
+            group, part = divmod(n, UNITS_PER_GROUP)
+            if part == 0:
+                res = res_pool.tile([P, HEADS, CHUNK, HEAD_DIM], F32, name="res")
+                res_tiles[group] = res
+            own_term, partner_term = term_tiles[n]
+            nc.gpsimd.tensor_tensor(
+                out=res_tiles[group][:, :, part * UNIT : (part + 1) * UNIT, :],
+                in0=own_term[:],
+                in1=partner_term[:],
+                op=ALU.add,
+            )
+
+        def store_group(group):
+            c, b = divmod(group, BATCH)
+            js = slice(c * CHUNK, (c + 1) * CHUNK)
+            res = res_tiles[group]
+            nc.sync.dma_start(out=q_view[b][:, :, js, :], in_=res[:, 0:Q_HEADS, :, :])
+            nc.sync.dma_start(out=k_view[b, 0][:, js, :], in_=res[:, Q_HEADS, :, :])
+
+        for n in range(-3, UNITS):
+            if 0 <= n + 1 < UNITS:
+                quantise_unit(n + 1)
+                project_unit(n + 1)
+            if n + 3 < UNITS:
+                transpose_unit(n + 3)
+                group, part = divmod(n + 3, UNITS_PER_GROUP)
+                if part == UNITS_PER_GROUP - 1 and group + X_BUFS < GROUPS:
+                    load_x(group + X_BUFS)
+                if part == 0 and group % BATCH == 0 and group > 0:
+                    build_tables(group // BATCH)
+                    if group // BATCH + 1 < CHUNKS:
+                        load_cos_sin(group // BATCH + 1)
+            if 0 <= n + 2 < UNITS:
+                regroup_unit(n + 2)
+            if 0 <= n + 1 < UNITS:
+                root_mean_square_unit(n + 1)
+            if n >= 0:
+                row_scale_unit(n)
+                rotary_terms_unit(n)
+                add_unit(n)
+                if n % UNITS_PER_GROUP == UNITS_PER_GROUP - 1:
+                    store_group(n // UNITS_PER_GROUP)

@@ -303,7 +303,7 @@ def tile_biboattention_pa_t_kernel(
                 res = res_pool.tile([P, HEADS, CHUNK, HEAD_DIM], F32, name="res")
                 res_tiles[group] = res
             own_term, partner_term = term_tiles[n]
-            nc.gpsimd.tensor_tensor(
+            nc.vector.tensor_tensor(
                 out=res_tiles[group][:, :, part * UNIT : (part + 1) * UNIT, :],
                 in0=own_term[:],
                 in1=partner_term[:],

@@ -36,7 +36,7 @@ GROUPS = CHUNKS * BATCH
 UNIT = 2
 UNITS_PER_GROUP = CHUNK // UNIT
 UNITS = GROUPS * UNITS_PER_GROUP
-X_BUFS = 4
+X_BUFS = 8
 
 FLOPS = 2 * BATCH * SEQ * HIDDEN * OUT_COLS
 
@@ -82,14 +82,18 @@ def tile_biboattention_pa_t_kernel(
         acc_tiles = {}
         rms_tiles = {}
         scale_tiles = {}
-        term_tiles = {}
         res_tiles = {}
 
-        def load_x(group):
+        def first_position(n):
+            group, part = divmod(n, UNITS_PER_GROUP)
             c, b = divmod(group, BATCH)
-            x_sb = x_pool.tile([P, CHUNK, HIDDEN], BF16, name="x_sb")
-            nc.sync.dma_start(out=x_sb[:], in_=x_view[b][:, c * CHUNK : (c + 1) * CHUNK, :])
-            x_tiles[group] = x_sb
+            return b, c * CHUNK + part * UNIT
+
+        def load_x(n):
+            b, j = first_position(n)
+            x_sb = x_pool.tile([P, UNIT, HIDDEN], BF16, name="x_sb")
+            nc.sync.dma_start(out=x_sb[:], in_=x_view[b][:, j : j + UNIT, :])
+            x_tiles[n] = x_sb
 
         load_x(0)
 
@@ -123,66 +127,46 @@ def tile_biboattention_pa_t_kernel(
         nc.vector.memset(eps_col[:], EPS)
 
         gain_bf = keep.tile([P, Q_HEADS], BF16, name="gain_bf")
-        nc.scalar.dma_start(
+        nc.gpsimd.dma_start(
             out=gain_bf[:], in_=ssmax_scale.rearrange("a h b c -> (a h b c)").partition_broadcast(P)
         )
         gain = keep.tile([P, HEADS], F32, name="gain")
         nc.vector.memset(gain[:], 1.0)
         nc.vector.tensor_scalar_mul(out=gain[:, 0:Q_HEADS], in0=gain_bf[:], scalar1=math.log(SEQ))
 
-        w_own = []
-        w_partner = []
-        for name, vec in (("q", q_norm_w), ("k", k_norm_w)):
-            own = keep.tile([P, HEAD_DIM], BF16, name="w_own_" + name)
-            nc.scalar.dma_start(out=own[:], in_=vec.partition_broadcast(P))
-            partner = keep.tile([P, HEAD_DIM], BF16, name="w_partner_" + name)
-            nc.vector.tensor_scalar_mul(out=partner[:, 0:HALF], in0=own[:, HALF:HEAD_DIM], scalar1=-1.0)
-            nc.vector.tensor_copy(out=partner[:, HALF:HEAD_DIM], in_=own[:, 0:HALF])
-            w_own.append(own)
-            w_partner.append(partner)
+        w4 = keep.tile([P, 2, 2, HEAD_DIM], BF16, name="w4")
+        nc.gpsimd.dma_start(out=w4[:, 0, 0, :], in_=q_norm_w.partition_broadcast(P))
+        nc.gpsimd.dma_start(out=w4[:, 0, 1, :], in_=k_norm_w.partition_broadcast(P))
+        nc.vector.tensor_scalar_mul(out=w4[:, 1, :, 0:HALF], in0=w4[:, 0, :, HALF:HEAD_DIM], scalar1=-1.0)
+        nc.vector.tensor_copy(out=w4[:, 1, :, HALF:HEAD_DIM], in_=w4[:, 0, :, 0:HALF])
 
-        cos_sb = keep.tile([P, POS_PER_PART, HEAD_DIM], BF16, name="cos_sb")
-        sin_sb = keep.tile([P, POS_PER_PART, HEAD_DIM], BF16, name="sin_sb")
-        cos_w = []
-        sin_w = []
-        for name in ("q", "k"):
-            cos_tab = keep.tile([P, POS_PER_PART, HEAD_DIM], F32, name="cos_w_" + name)
-            sin_tab = keep.tile([P, POS_PER_PART, HEAD_DIM], F32, name="sin_w_" + name)
-            cos_w.append(cos_tab)
-            sin_w.append(sin_tab)
+        cos_sin = keep.tile([P, POS_PER_PART, 2, HEAD_DIM], BF16, name="cos_sin")
+        table = keep.tile([P, POS_PER_PART, 2, 2, HEAD_DIM], F32, name="table")
 
-        def load_cos_sin(c):
-            js = slice(c * CHUNK, (c + 1) * CHUNK)
-            nc.scalar.dma_start(out=cos_sb[:, js, :], in_=cos_view[:, js, :])
-            nc.scalar.dma_start(out=sin_sb[:, js, :], in_=sin_view[:, js, :])
+        def build_table(j):
+            nc.vector.tensor_tensor(
+                out=table[:, j],
+                in0=cos_sin[:, j].unsqueeze(2).to_broadcast([P, 2, 2, HEAD_DIM]),
+                in1=w4[:],
+                op=ALU.mult,
+            )
 
-        def build_tables(c):
-            js = slice(c * CHUNK, (c + 1) * CHUNK)
-            for kind in range(2):
-                nc.gpsimd.tensor_tensor(
-                    out=cos_w[kind][:, js, :],
-                    in0=cos_sb[:, js, :],
-                    in1=w_own[kind][:].unsqueeze(1).to_broadcast([P, CHUNK, HEAD_DIM]),
-                    op=ALU.mult,
-                )
-                nc.gpsimd.tensor_tensor(
-                    out=sin_w[kind][:, js, :],
-                    in0=sin_sb[:, js, :],
-                    in1=w_partner[kind][:].unsqueeze(1).to_broadcast([P, CHUNK, HEAD_DIM]),
-                    op=ALU.mult,
-                )
-
-        load_cos_sin(0)
-        build_tables(0)
         load_x(1)
-        load_cos_sin(1)
-        for group in range(2, X_BUFS):
-            load_x(group)
+        load_x(2)
+        nc.sync.dma_start(out=cos_sin[:, 0:CHUNK, 0, :], in_=cos_view[:, 0:CHUNK, :])
+        nc.sync.dma_start(out=cos_sin[:, 0:CHUNK, 1, :], in_=sin_view[:, 0:CHUNK, :])
+        load_x(3)
+        load_x(4)
+        nc.sync.dma_start(out=cos_sin[:, CHUNK:POS_PER_PART, 0, :], in_=cos_view[:, CHUNK:POS_PER_PART, :])
+        nc.sync.dma_start(out=cos_sin[:, CHUNK:POS_PER_PART, 1, :], in_=sin_view[:, CHUNK:POS_PER_PART, :])
+        for n in range(5, X_BUFS):
+            load_x(n)
+        for j in range(CHUNK):
+            build_table(j)
 
         def transpose_unit(n):
-            group, part = divmod(n, UNITS_PER_GROUP)
             for t in range(UNIT):
-                words = x_tiles[group][:, part * UNIT + t, :].bitcast(F32)
+                words = x_tiles[n][:, t, :].bitcast(F32)
                 xt = psum_t.tile([P, PASSES * 2, P], F32, name="xt")
                 for g in range(PASSES):
                     for u in range(2):
@@ -258,57 +242,51 @@ def tile_biboattention_pa_t_kernel(
             )
             scale_tiles[n] = row_scale
 
-        def rotary_terms_unit(n):
+        def rotary_unit(n):
             group, part = divmod(n, UNITS_PER_GROUP)
-            c = group // BATCH
+            b, j = first_position(n)
+            if part == 0:
+                res = res_pool.tile([P, HEADS, CHUNK, HEAD_DIM], F32, name="res")
+                res_tiles[group] = res
             row_scale = scale_tiles[n]
-            own_term = work.tile([P, HEADS, UNIT, HEAD_DIM], F32, name="own_term")
-            partner_term = work.tile([P, HEADS, UNIT, HEAD_DIM], F32, name="partner_term")
+            own_term = work.tile([P, UNIT, HEADS, HEAD_DIM], F32, name="own_term")
+            partner_term = work.tile([P, UNIT, HEADS, HEAD_DIM], F32, name="partner_term")
             for t in range(UNIT):
-                j = c * CHUNK + part * UNIT + t
                 acc = acc_tiles[(n, t)]
                 for h in range(HEADS):
                     kind = 0 if h < Q_HEADS else 1
                     base = h * HEAD_DIM
                     factor = row_scale[:, h, t : t + 1]
                     nc.vector.scalar_tensor_tensor(
-                        out=own_term[:, h, t, :],
+                        out=own_term[:, t, h, :],
                         in0=acc[:, base : base + HEAD_DIM],
                         scalar=factor,
-                        in1=cos_w[kind][:, j, :],
+                        in1=table[:, j + t, 0, kind, :],
                         op0=ALU.mult,
                         op1=ALU.mult,
                     )
                     nc.vector.scalar_tensor_tensor(
-                        out=partner_term[:, h, t, 0:HALF],
+                        out=partner_term[:, t, h, 0:HALF],
                         in0=acc[:, base + HALF : base + HEAD_DIM],
                         scalar=factor,
-                        in1=sin_w[kind][:, j, 0:HALF],
+                        in1=table[:, j + t, 1, kind, 0:HALF],
                         op0=ALU.mult,
                         op1=ALU.mult,
                     )
                     nc.vector.scalar_tensor_tensor(
-                        out=partner_term[:, h, t, HALF:HEAD_DIM],
+                        out=partner_term[:, t, h, HALF:HEAD_DIM],
                         in0=acc[:, base : base + HALF],
                         scalar=factor,
-                        in1=sin_w[kind][:, j, HALF:HEAD_DIM],
+                        in1=table[:, j + t, 1, kind, HALF:HEAD_DIM],
                         op0=ALU.mult,
                         op1=ALU.mult,
                     )
-            term_tiles[n] = (own_term, partner_term)
-
-        def add_unit(n):
-            group, part = divmod(n, UNITS_PER_GROUP)
-            if part == 0:
-                res = res_pool.tile([P, HEADS, CHUNK, HEAD_DIM], F32, name="res")
-                res_tiles[group] = res
-            own_term, partner_term = term_tiles[n]
-            nc.vector.tensor_tensor(
-                out=res_tiles[group][:, :, part * UNIT : (part + 1) * UNIT, :],
-                in0=own_term[:],
-                in1=partner_term[:],
-                op=ALU.add,
-            )
+                nc.gpsimd.tensor_tensor(
+                    out=res_tiles[group][:, :, part * UNIT + t, :],
+                    in0=own_term[:, t],
+                    in1=partner_term[:, t],
+                    op=ALU.add,
+                )
 
         def store_group(group):
             c, b = divmod(group, BATCH)
@@ -317,26 +295,24 @@ def tile_biboattention_pa_t_kernel(
             nc.sync.dma_start(out=q_view[b][:, :, js, :], in_=res[:, 0:Q_HEADS, :, :])
             nc.sync.dma_start(out=k_view[b, 0][:, js, :], in_=res[:, Q_HEADS, :, :])
 
-        for n in range(-3, UNITS):
-            if 0 <= n + 1 < UNITS:
-                quantise_unit(n + 1)
-                project_unit(n + 1)
-            if n + 3 < UNITS:
-                transpose_unit(n + 3)
-                group, part = divmod(n + 3, UNITS_PER_GROUP)
-                if part == UNITS_PER_GROUP - 1 and group + X_BUFS < GROUPS:
-                    load_x(group + X_BUFS)
-                if part == 0 and group % BATCH == 0 and group > 0:
-                    build_tables(group // BATCH)
-                    if group // BATCH + 1 < CHUNKS:
-                        load_cos_sin(group // BATCH + 1)
+        for n in range(-4, UNITS):
+            if n >= 0:
+                row_scale_unit(n)
+            if n >= 0 and n % 2 == 0 and n // 2 + CHUNK < POS_PER_PART:
+                build_table(n // 2 + CHUNK)
             if 0 <= n + 2 < UNITS:
-                regroup_unit(n + 2)
+                quantise_unit(n + 2)
+            if 0 <= n + 1 < UNITS:
+                project_unit(n + 1)
+            if n + 4 < UNITS:
+                transpose_unit(n + 4)
+                if n + 4 + X_BUFS < UNITS:
+                    load_x(n + 4 + X_BUFS)
+            if 0 <= n + 3 < UNITS:
+                regroup_unit(n + 3)
             if 0 <= n + 1 < UNITS:
                 root_mean_square_unit(n + 1)
             if n >= 0:
-                row_scale_unit(n)
-                rotary_terms_unit(n)
-                add_unit(n)
+                rotary_unit(n)
                 if n % UNITS_PER_GROUP == UNITS_PER_GROUP - 1:
                     store_group(n // UNITS_PER_GROUP)

@@ -37,6 +37,8 @@ UNIT = 2
 UNITS_PER_GROUP = CHUNK // UNIT
 UNITS = GROUPS * UNITS_PER_GROUP
 X_BUFS = 8
+GAIN_COL = 2 * HEAD_DIM
+CONST_COLS = GAIN_COL + HEADS + 1
 
 FLOPS = 2 * BATCH * SEQ * HIDDEN * OUT_COLS
 
@@ -71,7 +73,8 @@ def tile_biboattention_pa_t_kernel(
         row_pool = ctx.enter_context(tc.tile_pool(name="row", bufs=3))
         work = ctx.enter_context(tc.tile_pool(name="work", bufs=3))
         res_pool = ctx.enter_context(tc.tile_pool(name="res", bufs=3))
-        psum_t = ctx.enter_context(tc.psum_pool(name="psum_t", bufs=2 * UNIT))
+        psum_c = ctx.enter_context(tc.psum_pool(name="psum_c", bufs=1))
+        psum_t = ctx.enter_context(tc.psum_pool(name="psum_t", bufs=3))
         psum_o = ctx.enter_context(tc.psum_pool(name="psum_o", bufs=2 * UNIT))
         ctx.enter_context(tc.manual_schedule())
 
@@ -83,6 +86,7 @@ def tile_biboattention_pa_t_kernel(
         rms_tiles = {}
         scale_tiles = {}
         res_tiles = {}
+        term_tiles = {}
 
         def first_position(n):
             group, part = divmod(n, UNITS_PER_GROUP)
@@ -126,43 +130,66 @@ def tile_biboattention_pa_t_kernel(
         eps_col = keep.tile([P, 1], F32, name="eps_col")
         nc.vector.memset(eps_col[:], EPS)
 
+        w_bf = keep.tile([P, 2, HEAD_DIM], BF16, name="w_bf")
+        nc.gpsimd.dma_start(out=w_bf[:, 0, :], in_=q_norm_w.partition_broadcast(P))
+        nc.gpsimd.dma_start(out=w_bf[:, 1, :], in_=k_norm_w.partition_broadcast(P))
         gain_bf = keep.tile([P, Q_HEADS], BF16, name="gain_bf")
         nc.gpsimd.dma_start(
             out=gain_bf[:], in_=ssmax_scale.rearrange("a h b c -> (a h b c)").partition_broadcast(P)
         )
-        gain = keep.tile([P, HEADS], F32, name="gain")
-        nc.vector.memset(gain[:], 1.0)
-        nc.vector.tensor_scalar_mul(out=gain[:, 0:Q_HEADS], in0=gain_bf[:], scalar1=math.log(SEQ))
+        const_sb = keep.tile([P, CONST_COLS], F32, name="const_sb")
+        nc.vector.memset(const_sb[:, GAIN_COL:CONST_COLS], 1.0)
+        nc.vector.tensor_copy(out=const_sb[:, 0:GAIN_COL], in_=w_bf[:].rearrange("p k d -> p (k d)"))
+        nc.vector.tensor_scalar_mul(
+            out=const_sb[:, GAIN_COL : GAIN_COL + Q_HEADS], in0=gain_bf[:], scalar1=math.log(SEQ)
+        )
+        const_ps = psum_c.tile([P, CONST_COLS], F32, name="const_ps")
+        w_ps = const_ps[:, 0:GAIN_COL].rearrange("p (k d) -> p k d", k=2)
+        gain_ps = const_ps[:, GAIN_COL : GAIN_COL + HEADS]
 
-        w4 = keep.tile([P, 2, 2, HEAD_DIM], BF16, name="w4")
-        nc.gpsimd.dma_start(out=w4[:, 0, 0, :], in_=q_norm_w.partition_broadcast(P))
-        nc.gpsimd.dma_start(out=w4[:, 0, 1, :], in_=k_norm_w.partition_broadcast(P))
-        nc.vector.tensor_scalar_mul(out=w4[:, 1, :, 0:HALF], in0=w4[:, 0, :, HALF:HEAD_DIM], scalar1=-1.0)
-        nc.vector.tensor_copy(out=w4[:, 1, :, HALF:HEAD_DIM], in_=w4[:, 0, :, 0:HALF])
+        def constants_to_psum():
+            nc.tensor.matmul(const_ps[:], lhsT=ident[:], rhs=const_sb[:], start=True, stop=True)
 
         cos_sin = keep.tile([P, POS_PER_PART, 2, HEAD_DIM], BF16, name="cos_sin")
         table = keep.tile([P, POS_PER_PART, 2, 2, HEAD_DIM], F32, name="table")
+
+        def load_cos_sin(js):
+            nc.sync.dma_start(out=cos_sin[:, js, 0, :], in_=cos_view[:, js, :])
+            nc.sync.dma_start(out=cos_sin[:, js, 1, 0:HALF], in_=sin_view[:, js, HALF:HEAD_DIM])
+            nc.sync.dma_start(out=cos_sin[:, js, 1, HALF:HEAD_DIM], in_=sin_view[:, js, 0:HALF])
+
+        def negate_sin(js):
+            nc.vector.tensor_scalar_mul(
+                out=cos_sin[:, js, 1, HALF:HEAD_DIM], in0=cos_sin[:, js, 1, HALF:HEAD_DIM], scalar1=-1.0
+            )
 
         def build_table(j):
             nc.vector.tensor_tensor(
                 out=table[:, j],
                 in0=cos_sin[:, j].unsqueeze(2).to_broadcast([P, 2, 2, HEAD_DIM]),
-                in1=w4[:],
+                in1=w_ps.unsqueeze(1).to_broadcast([P, 2, 2, HEAD_DIM]),
                 op=ALU.mult,
             )
 
         load_x(1)
         load_x(2)
-        nc.sync.dma_start(out=cos_sin[:, 0:CHUNK, 0, :], in_=cos_view[:, 0:CHUNK, :])
-        nc.sync.dma_start(out=cos_sin[:, 0:CHUNK, 1, :], in_=sin_view[:, 0:CHUNK, :])
+        load_cos_sin(slice(0, CHUNK))
         load_x(3)
         load_x(4)
-        nc.sync.dma_start(out=cos_sin[:, CHUNK:POS_PER_PART, 0, :], in_=cos_view[:, CHUNK:POS_PER_PART, :])
-        nc.sync.dma_start(out=cos_sin[:, CHUNK:POS_PER_PART, 1, :], in_=sin_view[:, CHUNK:POS_PER_PART, :])
+        load_cos_sin(slice(CHUNK, POS_PER_PART))
         for n in range(5, X_BUFS):
             load_x(n)
-        for j in range(CHUNK):
-            build_table(j)
+
+        def table_work(n):
+            if n == -2:
+                negate_sin(slice(0, CHUNK))
+            if n in (-2, -1):
+                build_table(2 * (n + 2))
+                build_table(2 * (n + 2) + 1)
+            if n == -1:
+                negate_sin(slice(CHUNK, POS_PER_PART))
+            if n >= 0 and n % 2 == 0 and n // 2 + CHUNK < POS_PER_PART:
+                build_table(n // 2 + CHUNK)
 
         def transpose_unit(n):
             for t in range(UNIT):
@@ -185,15 +212,18 @@ def tile_biboattention_pa_t_kernel(
                 )
             grouped_tiles[n] = grouped
 
-        def quantise_unit(n):
-            x_codes = mx_pool.tile([P, UNIT * PASSES * P], U32, name="x_codes", align_bytes=64)
-            x_scales = mx_pool.tile([P, UNIT * PASSES * P], U8, name="x_scales", align_bytes=64)
+        def quantise_tile(n, t):
+            if t == 0:
+                x_codes = mx_pool.tile([P, UNIT * PASSES * P], U32, name="x_codes", align_bytes=64)
+                x_scales = mx_pool.tile([P, UNIT * PASSES * P], U8, name="x_scales", align_bytes=64)
+                code_tiles[n] = (x_codes, x_scales)
+            x_codes, x_scales = code_tiles[n]
+            words = slice(t * PASSES * P, (t + 1) * PASSES * P)
             nc.vector.quantize_mx(
-                out=x_codes[:].bitcast(FP8X4),
-                scales=x_scales[:],
-                in_=grouped_tiles[n][:].rearrange("p t c -> p (t c)"),
+                out=x_codes[:, words].bitcast(FP8X4),
+                scales=x_scales[:, words],
+                in_=grouped_tiles[n][:, t, :],
             )
-            code_tiles[n] = (x_codes, x_scales)
 
         def project_unit(n):
             x_codes, x_scales = code_tiles[n]
@@ -226,67 +256,67 @@ def tile_biboattention_pa_t_kernel(
                     )
             rms = row_pool.tile([P, HEADS, UNIT], F32, name="rms")
             nc.scalar.activation(
-                out=rms[:], in_=sumsq[:], func=ACT.Sqrt, scale=1.0 / HEAD_DIM, bias=eps_col[:, 0:1]
+                out=rms[:], in_=sumsq[:], func=ACT.Abs_reciprocal_sqrt, scale=1.0 / HEAD_DIM, bias=eps_col[:, 0:1]
             )
             rms_tiles[n] = rms
 
         def row_scale_unit(n):
-            inv_rms = row_pool.tile([P, HEADS, UNIT], F32, name="inv_rms")
-            nc.vector.reciprocal(out=inv_rms[:], in_=rms_tiles[n][:])
             row_scale = row_pool.tile([P, HEADS, UNIT], F32, name="row_scale")
             nc.vector.tensor_tensor(
                 out=row_scale[:],
-                in0=inv_rms[:],
-                in1=gain[:].unsqueeze(2).to_broadcast([P, HEADS, UNIT]),
+                in0=rms_tiles[n][:],
+                in1=gain_ps.unsqueeze(2).to_broadcast([P, HEADS, UNIT]),
                 op=ALU.mult,
             )
             scale_tiles[n] = row_scale
 
-        def rotary_unit(n):
+        def rotary_tile(n, t):
             group, part = divmod(n, UNITS_PER_GROUP)
             b, j = first_position(n)
-            if part == 0:
+            if part == 0 and t == 0:
                 res = res_pool.tile([P, HEADS, CHUNK, HEAD_DIM], F32, name="res")
                 res_tiles[group] = res
+            if t == 0:
+                own_term = work.tile([P, UNIT, HEADS, HEAD_DIM], F32, name="own_term")
+                partner_term = work.tile([P, UNIT, HEADS, HEAD_DIM], F32, name="partner_term")
+                term_tiles[n] = (own_term, partner_term)
+            own_term, partner_term = term_tiles[n]
             row_scale = scale_tiles[n]
-            own_term = work.tile([P, UNIT, HEADS, HEAD_DIM], F32, name="own_term")
-            partner_term = work.tile([P, UNIT, HEADS, HEAD_DIM], F32, name="partner_term")
-            for t in range(UNIT):
-                acc = acc_tiles[(n, t)]
-                for h in range(HEADS):
-                    kind = 0 if h < Q_HEADS else 1
-                    base = h * HEAD_DIM
-                    factor = row_scale[:, h, t : t + 1]
-                    nc.vector.scalar_tensor_tensor(
-                        out=own_term[:, t, h, :],
-                        in0=acc[:, base : base + HEAD_DIM],
-                        scalar=factor,
-                        in1=table[:, j + t, 0, kind, :],
-                        op0=ALU.mult,
-                        op1=ALU.mult,
-                    )
-                    nc.vector.scalar_tensor_tensor(
-                        out=partner_term[:, t, h, 0:HALF],
-                        in0=acc[:, base + HALF : base + HEAD_DIM],
-                        scalar=factor,
-                        in1=table[:, j + t, 1, kind, 0:HALF],
-                        op0=ALU.mult,
-                        op1=ALU.mult,
-                    )
-                    nc.vector.scalar_tensor_tensor(
-                        out=partner_term[:, t, h, HALF:HEAD_DIM],
-                        in0=acc[:, base : base + HALF],
-                        scalar=factor,
-                        in1=table[:, j + t, 1, kind, HALF:HEAD_DIM],
-                        op0=ALU.mult,
-                        op1=ALU.mult,
-                    )
-                nc.gpsimd.tensor_tensor(
-                    out=res_tiles[group][:, :, part * UNIT + t, :],
-                    in0=own_term[:, t],
-                    in1=partner_term[:, t],
-                    op=ALU.add,
+            acc = acc_tiles[(n, t)]
+            for h in range(HEADS):
+                kind = 0 if h < Q_HEADS else 1
+                base = h * HEAD_DIM
+                factor = row_scale[:, h, t : t + 1]
+                nc.vector.scalar_tensor_tensor(
+                    out=own_term[:, t, h, :],
+                    in0=acc[:, base : base + HEAD_DIM],
+                    scalar=factor,
+                    in1=table[:, j + t, 0, kind, :],
+                    op0=ALU.mult,
+                    op1=ALU.mult,
                 )
+                nc.vector.scalar_tensor_tensor(
+                    out=partner_term[:, t, h, HALF:HEAD_DIM],
+                    in0=acc[:, base : base + HALF],
+                    scalar=factor,
+                    in1=table[:, j + t, 1, kind, 0:HALF],
+                    op0=ALU.mult,
+                    op1=ALU.mult,
+                )
+                nc.vector.scalar_tensor_tensor(
+                    out=partner_term[:, t, h, 0:HALF],
+                    in0=acc[:, base + HALF : base + HEAD_DIM],
+                    scalar=factor,
+                    in1=table[:, j + t, 1, kind, HALF:HEAD_DIM],
+                    op0=ALU.mult,
+                    op1=ALU.mult,
+                )
+            nc.gpsimd.tensor_tensor(
+                out=res_tiles[group][:, :, part * UNIT + t, :],
+                in0=own_term[:, t],
+                in1=partner_term[:, t],
+                op=ALU.add,
+            )
 
         def store_group(group):
             c, b = divmod(group, BATCH)
@@ -296,23 +326,27 @@ def tile_biboattention_pa_t_kernel(
             nc.sync.dma_start(out=k_view[b, 0][:, js, :], in_=res[:, Q_HEADS, :, :])
 
         for n in range(-4, UNITS):
-            if n >= 0:
-                row_scale_unit(n)
-            if n >= 0 and n % 2 == 0 and n // 2 + CHUNK < POS_PER_PART:
-                build_table(n // 2 + CHUNK)
-            if 0 <= n + 2 < UNITS:
-                quantise_unit(n + 2)
-            if 0 <= n + 1 < UNITS:
-                project_unit(n + 1)
-            if n + 4 < UNITS:
-                transpose_unit(n + 4)
-                if n + 4 + X_BUFS < UNITS:
-                    load_x(n + 4 + X_BUFS)
-            if 0 <= n + 3 < UNITS:
-                regroup_unit(n + 3)
-            if 0 <= n + 1 < UNITS:
-                root_mean_square_unit(n + 1)
-            if n >= 0:
-                rotary_unit(n)
-                if n % UNITS_PER_GROUP == UNITS_PER_GROUP - 1:
-                    store_group(n // UNITS_PER_GROUP)
+            for t in range(UNIT):
+                if 0 <= n + 2 < UNITS:
+                    quantise_tile(n + 2, t)
+                if n >= 0 and t == 0:
+                    row_scale_unit(n)
+                if t == 1:
+                    table_work(n)
+                if t == 0:
+                    if 0 <= n + 1 < UNITS:
+                        project_unit(n + 1)
+                    if 0 <= n + 3 < UNITS:
+                        regroup_unit(n + 3)
+                    if n + 4 < UNITS:
+                        transpose_unit(n + 4)
+                        if n == -3:
+                            constants_to_psum()
+                        if n + 4 + X_BUFS < UNITS:
+                            load_x(n + 4 + X_BUFS)
+                    if 0 <= n + 1 < UNITS:
+                        root_mean_square_unit(n + 1)
+                if n >= 0:
+                    rotary_tile(n, t)
+            if n >= 0 and n % UNITS_PER_GROUP == UNITS_PER_GROUP - 1:
+                store_group(n // UNITS_PER_GROUP)

@@ -296,18 +296,10 @@ def tile_biboattention_pa_t_kernel(
                     op1=ALU.mult,
                 )
                 nc.vector.scalar_tensor_tensor(
-                    out=partner_term[:, t, h, HALF:HEAD_DIM],
-                    in0=acc[:, base : base + HALF],
+                    out=partner_term[:, t, h, :].rearrange("p (a d) -> p a d", a=2),
+                    in0=acc[:, base : base + HEAD_DIM].rearrange("p (a d) -> p a d", a=2)[:, ::-1, :],
                     scalar=factor,
-                    in1=table[:, j + t, 1, kind, 0:HALF],
-                    op0=ALU.mult,
-                    op1=ALU.mult,
-                )
-                nc.vector.scalar_tensor_tensor(
-                    out=partner_term[:, t, h, 0:HALF],
-                    in0=acc[:, base + HALF : base + HEAD_DIM],
-                    scalar=factor,
-                    in1=table[:, j + t, 1, kind, HALF:HEAD_DIM],
+                    in1=table[:, j + t, 1, kind, :].rearrange("p (a d) -> p a d", a=2)[:, ::-1, :],
                     op0=ALU.mult,
                     op1=ALU.mult,
                 )

@@ -319,10 +319,10 @@ def tile_biboattention_pa_t_kernel(
 
         for n in range(-4, UNITS):
             for t in range(UNIT):
-                if 0 <= n + 2 < UNITS:
-                    quantise_tile(n + 2, t)
                 if n >= 0 and t == 0:
                     row_scale_unit(n)
+                if 0 <= n + 2 < UNITS:
+                    quantise_tile(n + 2, t)
                 if t == 1:
                     table_work(n)
                 if t == 0:

@@ -38,7 +38,7 @@ UNITS_PER_GROUP = CHUNK // UNIT
 UNITS = GROUPS * UNITS_PER_GROUP
 X_BUFS = 8
 GAIN_COL = 2 * HEAD_DIM
-CONST_COLS = GAIN_COL + HEADS + 1
+CONST_COLS = GAIN_COL + Q_HEADS
 
 FLOPS = 2 * BATCH * SEQ * HIDDEN * OUT_COLS
 
@@ -99,6 +99,27 @@ def tile_biboattention_pa_t_kernel(
             nc.sync.dma_start(out=x_sb[:], in_=x_view[b][:, j : j + UNIT, :])
             x_tiles[n] = x_sb
 
+        const_rows = keep.tile([P, CONST_COLS], BF16, name="const_rows")
+        nc.vector.memset(const_rows[:], 0.0)
+        nc.sync.dma_start(out=const_rows[0:1, 0:HEAD_DIM], in_=q_norm_w.rearrange("(o d) -> o d", o=1))
+        nc.sync.dma_start(out=const_rows[0:1, HEAD_DIM:GAIN_COL], in_=k_norm_w.rearrange("(o d) -> o d", o=1))
+        nc.sync.dma_start(out=const_rows[0:1, GAIN_COL:CONST_COLS], in_=ssmax_scale.rearrange("a h b c -> a (h b c)"))
+        ones = keep.tile([P, P], BF16, name="ones")
+        nc.vector.memset(ones[:], 1.0)
+        const_ps = psum_c.tile([P, CONST_COLS], F32, name="const_ps")
+        nc.tensor.matmul(const_ps[:], lhsT=ones[:], rhs=const_rows[:], start=True, stop=True)
+        w_ps = const_ps[:, 0:GAIN_COL].rearrange("p (k d) -> p k d", k=2)
+        gain_ps = const_ps[:, GAIN_COL:CONST_COLS]
+
+        cos_sin = keep.tile([P, POS_PER_PART, 2, HEAD_DIM], BF16, name="cos_sin")
+        table = keep.tile([P, POS_PER_PART, 2, 2, HEAD_DIM], F32, name="table")
+
+        def load_cos_sin(js):
+            nc.sync.dma_start(out=cos_sin[:, js, 0, :], in_=cos_view[:, js, :])
+            nc.sync.dma_start(out=cos_sin[:, js, 1, 0:HALF], in_=sin_view[:, js, HALF:HEAD_DIM])
+            nc.sync.dma_start(out=cos_sin[:, js, 1, HALF:HEAD_DIM], in_=sin_view[:, js, 0:HALF])
+
+        load_cos_sin(slice(0, CHUNK))
         load_x(0)
 
         w_codes = keep.tile([P, PASSES, OUT_COLS], U32, name="w_codes", align_bytes=64)
@@ -130,34 +151,6 @@ def tile_biboattention_pa_t_kernel(
         eps_col = keep.tile([P, 1], F32, name="eps_col")
         nc.vector.memset(eps_col[:], EPS)
 
-        w_bf = keep.tile([P, 2, HEAD_DIM], BF16, name="w_bf")
-        nc.gpsimd.dma_start(out=w_bf[:, 0, :], in_=q_norm_w.partition_broadcast(P))
-        nc.gpsimd.dma_start(out=w_bf[:, 1, :], in_=k_norm_w.partition_broadcast(P))
-        gain_bf = keep.tile([P, Q_HEADS], BF16, name="gain_bf")
-        nc.gpsimd.dma_start(
-            out=gain_bf[:], in_=ssmax_scale.rearrange("a h b c -> (a h b c)").partition_broadcast(P)
-        )
-        const_sb = keep.tile([P, CONST_COLS], F32, name="const_sb")
-        nc.vector.memset(const_sb[:, GAIN_COL:CONST_COLS], 1.0)
-        nc.vector.tensor_copy(out=const_sb[:, 0:GAIN_COL], in_=w_bf[:].rearrange("p k d -> p (k d)"))
-        nc.vector.tensor_scalar_mul(
-            out=const_sb[:, GAIN_COL : GAIN_COL + Q_HEADS], in0=gain_bf[:], scalar1=math.log(SEQ)
-        )
-        const_ps = psum_c.tile([P, CONST_COLS], F32, name="const_ps")
-        w_ps = const_ps[:, 0:GAIN_COL].rearrange("p (k d) -> p k d", k=2)
-        gain_ps = const_ps[:, GAIN_COL : GAIN_COL + HEADS]
-
-        def constants_to_psum():
-            nc.tensor.matmul(const_ps[:], lhsT=ident[:], rhs=const_sb[:], start=True, stop=True)
-
-        cos_sin = keep.tile([P, POS_PER_PART, 2, HEAD_DIM], BF16, name="cos_sin")
-        table = keep.tile([P, POS_PER_PART, 2, 2, HEAD_DIM], F32, name="table")
-
-        def load_cos_sin(js):
-            nc.sync.dma_start(out=cos_sin[:, js, 0, :], in_=cos_view[:, js, :])
-            nc.sync.dma_start(out=cos_sin[:, js, 1, 0:HALF], in_=sin_view[:, js, HALF:HEAD_DIM])
-            nc.sync.dma_start(out=cos_sin[:, js, 1, HALF:HEAD_DIM], in_=sin_view[:, js, 0:HALF])
-
         def negate_sin(js):
             nc.vector.tensor_scalar_mul(
                 out=cos_sin[:, js, 1, HALF:HEAD_DIM], in0=cos_sin[:, js, 1, HALF:HEAD_DIM], scalar1=-1.0
@@ -173,23 +166,27 @@ def tile_biboattention_pa_t_kernel(
 
         load_x(1)
         load_x(2)
-        load_cos_sin(slice(0, CHUNK))
+        load_cos_sin(slice(CHUNK, 2 * CHUNK))
         load_x(3)
         load_x(4)
-        load_cos_sin(slice(CHUNK, POS_PER_PART))
+        load_cos_sin(slice(2 * CHUNK, POS_PER_PART))
         for n in range(5, X_BUFS):
             load_x(n)
 
+        negate_sin(slice(0, CHUNK))
+        for j in range(CHUNK):
+            build_table(j)
+
         def table_work(n):
             if n == -2:
-                negate_sin(slice(0, CHUNK))
+                negate_sin(slice(CHUNK, 2 * CHUNK))
             if n in (-2, -1):
-                build_table(2 * (n + 2))
-                build_table(2 * (n + 2) + 1)
+                build_table(CHUNK + 2 * (n + 2))
+                build_table(CHUNK + 2 * (n + 2) + 1)
             if n == -1:
-                negate_sin(slice(CHUNK, POS_PER_PART))
-            if n >= 0 and n % 2 == 0 and n // 2 + CHUNK < POS_PER_PART:
-                build_table(n // 2 + CHUNK)
+                negate_sin(slice(2 * CHUNK, POS_PER_PART))
+            if n >= 0 and n % 2 == 0 and n // 2 + 2 * CHUNK < POS_PER_PART:
+                build_table(n // 2 + 2 * CHUNK)
 
         def transpose_unit(n):
             for t in range(UNIT):
@@ -261,12 +258,14 @@ def tile_biboattention_pa_t_kernel(
             rms_tiles[n] = rms
 
         def row_scale_unit(n):
-            row_scale = row_pool.tile([P, HEADS, UNIT], F32, name="row_scale")
-            nc.vector.tensor_tensor(
+            row_scale = row_pool.tile([P, Q_HEADS, UNIT], F32, name="row_scale")
+            nc.vector.scalar_tensor_tensor(
                 out=row_scale[:],
-                in0=rms_tiles[n][:],
-                in1=gain_ps.unsqueeze(2).to_broadcast([P, HEADS, UNIT]),
-                op=ALU.mult,
+                in0=rms_tiles[n][:, 0:Q_HEADS, :],
+                scalar=math.log(SEQ),
+                in1=gain_ps.unsqueeze(2).to_broadcast([P, Q_HEADS, UNIT]),
+                op0=ALU.mult,
+                op1=ALU.mult,
             )
             scale_tiles[n] = row_scale
 
@@ -286,7 +285,7 @@ def tile_biboattention_pa_t_kernel(
             for h in range(HEADS):
                 kind = 0 if h < Q_HEADS else 1
                 base = h * HEAD_DIM
-                factor = row_scale[:, h, t : t + 1]
+                factor = row_scale[:, h, t : t + 1] if h < Q_HEADS else rms_tiles[n][:, h, t : t + 1]
                 nc.vector.scalar_tensor_tensor(
                     out=own_term[:, t, h, :],
                     in0=acc[:, base : base + HEAD_DIM],
@@ -310,35 +309,47 @@ def tile_biboattention_pa_t_kernel(
                 op=ALU.add,
             )
 
-        def store_group(group):
+        def store(group, first, count):
             c, b = divmod(group, BATCH)
-            js = slice(c * CHUNK, (c + 1) * CHUNK)
+            js = slice(c * CHUNK + first, c * CHUNK + first + count)
             res = res_tiles[group]
-            nc.sync.dma_start(out=q_view[b][:, :, js, :], in_=res[:, 0:Q_HEADS, :, :])
-            nc.sync.dma_start(out=k_view[b, 0][:, js, :], in_=res[:, Q_HEADS, :, :])
+            nc.sync.dma_start(out=q_view[b][:, :, js, :], in_=res[:, 0:Q_HEADS, first : first + count, :])
+            nc.sync.dma_start(out=k_view[b, 0][:, js, :], in_=res[:, Q_HEADS, first : first + count, :])
 
-        for n in range(-4, UNITS):
+        for n in range(-4, 0):
+            if n + 2 >= 0:
+                for t in range(UNIT):
+                    quantise_tile(n + 2, t)
+                project_unit(n + 2)
+            if n + 3 >= 0:
+                regroup_unit(n + 3)
+            transpose_unit(n + 4)
+            load_x(n + 4 + X_BUFS)
+            if n + 2 >= 0:
+                root_mean_square_unit(n + 2)
+            table_work(n)
+        for n in range(UNITS):
             for t in range(UNIT):
-                if n >= 0 and t == 0:
+                if t == 0:
                     row_scale_unit(n)
-                if 0 <= n + 2 < UNITS:
+                if n + 2 < UNITS:
                     quantise_tile(n + 2, t)
                 if t == 1:
                     table_work(n)
                 if t == 0:
-                    if 0 <= n + 1 < UNITS:
+                    if 1 <= n < UNITS - 1:
                         project_unit(n + 1)
-                    if 0 <= n + 3 < UNITS:
+                    if n + 3 < UNITS:
                         regroup_unit(n + 3)
                     if n + 4 < UNITS:
                         transpose_unit(n + 4)
-                        if n == -3:
-                            constants_to_psum()
                         if n + 4 + X_BUFS < UNITS:
                             load_x(n + 4 + X_BUFS)
-                    if 0 <= n + 1 < UNITS:
+                    if 1 <= n < UNITS - 1:
                         root_mean_square_unit(n + 1)
-                if n >= 0:
-                    rotary_tile(n, t)
-            if n >= 0 and n % UNITS_PER_GROUP == UNITS_PER_GROUP - 1:
-                store_group(n // UNITS_PER_GROUP)
+                rotary_tile(n, t)
+            group, part = divmod(n, UNITS_PER_GROUP)
+            if group == GROUPS - 1:
+                store(group, part * UNIT, UNIT)
+            elif part == UNITS_PER_GROUP - 1:
+                store(group, 0, CHUNK)

@@ -302,7 +302,8 @@ def tile_biboattention_pa_t_kernel(
                     op0=ALU.mult,
                     op1=ALU.mult,
                 )
-            nc.gpsimd.tensor_tensor(
+            adder = nc.vector if (n, t) == (UNITS - 1, UNIT - 1) else nc.gpsimd
+            adder.tensor_tensor(
                 out=res_tiles[group][:, :, part * UNIT + t, :],
                 in0=own_term[:, t],
                 in1=partner_term[:, t],
@@ -348,8 +349,10 @@ def tile_biboattention_pa_t_kernel(
                     if 1 <= n < UNITS - 1:
                         root_mean_square_unit(n + 1)
                 rotary_tile(n, t)
+                if n == UNITS - 1:
+                    store(GROUPS - 1, CHUNK - UNIT + t, 1)
             group, part = divmod(n, UNITS_PER_GROUP)
-            if group == GROUPS - 1:
-                store(group, part * UNIT, UNIT)
-            elif part == UNITS_PER_GROUP - 1:
+            if n == UNITS - 2:
+                store(group, 0, UNIT)
+            elif group < GROUPS - 1 and part == UNITS_PER_GROUP - 1:
                 store(group, 0, CHUNK)

@@ -99,6 +99,20 @@ def tile_biboattention_pa_t_kernel(
             nc.sync.dma_start(out=x_sb[:], in_=x_view[b][:, j : j + UNIT, :])
             x_tiles[n] = x_sb
 
+        w_scales = keep.tile([P, PASSES, OUT_COLS], U8, name="w_scales", align_bytes=64)
+        nc.vector.memset(w_scales[:].bitcast(I32), 0)
+        for quad in range(4):
+            rows = slice(4 * quad, 4 * quad + 4)
+            parts = slice(32 * quad, 32 * quad + 4)
+            nc.sync.dma_start(
+                out=w_scales[parts, :, 0:Q_COLS].bitcast(I32),
+                in_=wq_scales[:, rows, :].rearrange("g r n -> r g n").bitcast(I32),
+            )
+            nc.sync.dma_start(
+                out=w_scales[parts, :, Q_COLS:OUT_COLS].bitcast(I32),
+                in_=wk_scales[:, rows, :].rearrange("g r n -> r g n").bitcast(I32),
+            )
+
         const_rows = keep.tile([P, CONST_COLS], BF16, name="const_rows")
         nc.vector.memset(const_rows[:], 0.0)
         nc.sync.dma_start(out=const_rows[0:1, 0:HEAD_DIM], in_=q_norm_w.rearrange("(o d) -> o d", o=1))
@@ -131,20 +145,6 @@ def tile_biboattention_pa_t_kernel(
             out=w_codes[:, :, Q_COLS:OUT_COLS].bitcast(I32),
             in_=wk_words.rearrange("g p n t -> p g (n t)").bitcast(I32),
         )
-        w_scales = keep.tile([P, PASSES, OUT_COLS], U8, name="w_scales", align_bytes=64)
-        nc.vector.memset(w_scales[:].bitcast(I32), 0)
-        for quad in range(4):
-            rows = slice(4 * quad, 4 * quad + 4)
-            parts = slice(32 * quad, 32 * quad + 4)
-            nc.sync.dma_start(
-                out=w_scales[parts, :, 0:Q_COLS].bitcast(I32),
-                in_=wq_scales[:, rows, :].rearrange("g r n -> r g n").bitcast(I32),
-            )
-            nc.sync.dma_start(
-                out=w_scales[parts, :, Q_COLS:OUT_COLS].bitcast(I32),
-                in_=wk_scales[:, rows, :].rearrange("g r n -> r g n").bitcast(I32),
-            )
-
         ident = keep.tile([P, P], F32, name="ident")
         make_identity(nc, ident[:])
 

@@ -209,17 +209,14 @@ def tile_biboattention_pa_t_kernel(
                 )
             grouped_tiles[n] = grouped
 
-        def quantise_tile(n, t):
-            if t == 0:
-                x_codes = mx_pool.tile([P, UNIT * PASSES * P], U32, name="x_codes", align_bytes=64)
-                x_scales = mx_pool.tile([P, UNIT * PASSES * P], U8, name="x_scales", align_bytes=64)
-                code_tiles[n] = (x_codes, x_scales)
-            x_codes, x_scales = code_tiles[n]
-            words = slice(t * PASSES * P, (t + 1) * PASSES * P)
+        def quantise_unit(n):
+            x_codes = mx_pool.tile([P, UNIT * PASSES * P], U32, name="x_codes", align_bytes=64)
+            x_scales = mx_pool.tile([P, UNIT * PASSES * P], U8, name="x_scales", align_bytes=64)
+            code_tiles[n] = (x_codes, x_scales)
             nc.vector.quantize_mx(
-                out=x_codes[:, words].bitcast(FP8X4),
-                scales=x_scales[:, words],
-                in_=grouped_tiles[n][:, t, :],
+                out=x_codes[:].bitcast(FP8X4),
+                scales=x_scales[:],
+                in_=grouped_tiles[n][:].rearrange("p t k -> p (t k)"),
             )
 
         def project_unit(n):
@@ -276,8 +273,8 @@ def tile_biboattention_pa_t_kernel(
                 res = res_pool.tile([P, HEADS, CHUNK, HEAD_DIM], F32, name="res")
                 res_tiles[group] = res
             if t == 0:
-                own_term = work.tile([P, UNIT, HEADS, HEAD_DIM], F32, name="own_term")
-                partner_term = work.tile([P, UNIT, HEADS, HEAD_DIM], F32, name="partner_term")
+                own_term = work.tile([P, HEADS, UNIT, HEAD_DIM], F32, name="own_term")
+                partner_term = work.tile([P, HEADS, UNIT, HEAD_DIM], F32, name="partner_term")
                 term_tiles[n] = (own_term, partner_term)
             own_term, partner_term = term_tiles[n]
             row_scale = scale_tiles[n]
@@ -287,7 +284,7 @@ def tile_biboattention_pa_t_kernel(
                 base = h * HEAD_DIM
                 factor = row_scale[:, h, t : t + 1] if h < Q_HEADS else rms_tiles[n][:, h, t : t + 1]
                 nc.vector.scalar_tensor_tensor(
-                    out=own_term[:, t, h, :],
+                    out=own_term[:, h, t, :],
                     in0=acc[:, base : base + HEAD_DIM],
                     scalar=factor,
                     in1=table[:, j + t, 0, kind, :],
@@ -295,20 +292,29 @@ def tile_biboattention_pa_t_kernel(
                     op1=ALU.mult,
                 )
                 nc.vector.scalar_tensor_tensor(
-                    out=partner_term[:, t, h, :].rearrange("p (a d) -> p a d", a=2),
+                    out=partner_term[:, h, t, :].rearrange("p (a d) -> p a d", a=2),
                     in0=acc[:, base : base + HEAD_DIM].rearrange("p (a d) -> p a d", a=2)[:, ::-1, :],
                     scalar=factor,
                     in1=table[:, j + t, 1, kind, :].rearrange("p (a d) -> p a d", a=2)[:, ::-1, :],
                     op0=ALU.mult,
                     op1=ALU.mult,
                 )
-            adder = nc.vector if (n, t) == (UNITS - 1, UNIT - 1) else nc.gpsimd
-            adder.tensor_tensor(
-                out=res_tiles[group][:, :, part * UNIT + t, :],
-                in0=own_term[:, t],
-                in1=partner_term[:, t],
-                op=ALU.add,
-            )
+            if n < UNITS - 1:
+                if t == UNIT - 1:
+                    nc.gpsimd.tensor_tensor(
+                        out=res_tiles[group][:, :, part * UNIT : (part + 1) * UNIT, :],
+                        in0=own_term[:],
+                        in1=partner_term[:],
+                        op=ALU.add,
+                    )
+            else:
+                adder = nc.vector if t == UNIT - 1 else nc.gpsimd
+                adder.tensor_tensor(
+                    out=res_tiles[group][:, :, part * UNIT + t, :],
+                    in0=own_term[:, :, t, :],
+                    in1=partner_term[:, :, t, :],
+                    op=ALU.add,
+                )
 
         def store(group, first, count):
             c, b = divmod(group, BATCH)
@@ -319,8 +325,7 @@ def tile_biboattention_pa_t_kernel(
 
         for n in range(-4, 0):
             if n + 2 >= 0:
-                for t in range(UNIT):
-                    quantise_tile(n + 2, t)
+                quantise_unit(n + 2)
                 project_unit(n + 2)
             if n + 3 >= 0:
                 regroup_unit(n + 3)
@@ -333,8 +338,8 @@ def tile_biboattention_pa_t_kernel(
             for t in range(UNIT):
                 if t == 0:
                     row_scale_unit(n)
-                if n + 2 < UNITS:
-                    quantise_tile(n + 2, t)
+                if n + 2 < UNITS and t == 0:
+                    quantise_unit(n + 2)
                 if t == 1:
                     table_work(n)
                 if t == 0:

@@ -99,6 +99,39 @@ def tile_biboattention_pa_t_kernel(
             nc.sync.dma_start(out=x_sb[:], in_=x_view[b][:, j : j + UNIT, :])
             x_tiles[n] = x_sb
 
+        cos_t = keep.tile([P, POS_PER_PART, HEAD_DIM], BF16, name="cos_t")
+        sin_t = keep.tile([P, POS_PER_PART, HEAD_DIM], BF16, name="sin_t")
+
+        def load_cos_sin(js):
+            nc.sync.dma_start(out=cos_t[:, js, :], in_=cos_view[:, js, :])
+            nc.sync.dma_start(out=sin_t[:, js, :], in_=sin_view[:, js, :])
+
+        load_cos_sin(slice(0, 2 * CHUNK))
+
+        const_rows = keep.tile([P, CONST_COLS], BF16, name="const_rows")
+        nc.gpsimd.memset(const_rows[:], 0.0)
+        nc.sync.dma_start(out=const_rows[0:1, 0:HEAD_DIM], in_=q_norm_w.rearrange("(o d) -> o d", o=1))
+        nc.sync.dma_start(out=const_rows[0:1, HEAD_DIM:GAIN_COL], in_=k_norm_w.rearrange("(o d) -> o d", o=1))
+        nc.sync.dma_start(out=const_rows[0:1, GAIN_COL:CONST_COLS], in_=ssmax_scale.rearrange("a h b c -> a (h b c)"))
+        ones = keep.tile([P, P], BF16, name="ones")
+        nc.vector.memset(ones[:], 1.0)
+        const_ps = psum_c.tile([P, CONST_COLS], F32, name="const_ps")
+        nc.tensor.matmul(const_ps[:], lhsT=ones[:], rhs=const_rows[:], start=True, stop=True)
+        w_ps = const_ps[:, 0:GAIN_COL].rearrange("p (k d) -> p k d", k=2)
+        gain_ps = const_ps[:, GAIN_COL:CONST_COLS]
+
+        load_x(0)
+
+        w_codes = keep.tile([P, PASSES, OUT_COLS], U32, name="w_codes", align_bytes=64)
+        nc.sync.dma_start(
+            out=w_codes[:, :, 0:Q_COLS].bitcast(I32),
+            in_=wq_words.rearrange("g p n t -> p g (n t)").bitcast(I32),
+        )
+        nc.sync.dma_start(
+            out=w_codes[:, :, Q_COLS:OUT_COLS].bitcast(I32),
+            in_=wk_words.rearrange("g p n t -> p g (n t)").bitcast(I32),
+        )
+
         w_scales = keep.tile([P, PASSES, OUT_COLS], U8, name="w_scales", align_bytes=64)
         nc.vector.memset(w_scales[:].bitcast(I32), 0)
         for quad in range(4):
@@ -113,80 +146,43 @@ def tile_biboattention_pa_t_kernel(
                 in_=wk_scales[:, rows, :].rearrange("g r n -> r g n").bitcast(I32),
             )
 
-        const_rows = keep.tile([P, CONST_COLS], BF16, name="const_rows")
-        nc.vector.memset(const_rows[:], 0.0)
-        nc.sync.dma_start(out=const_rows[0:1, 0:HEAD_DIM], in_=q_norm_w.rearrange("(o d) -> o d", o=1))
-        nc.sync.dma_start(out=const_rows[0:1, HEAD_DIM:GAIN_COL], in_=k_norm_w.rearrange("(o d) -> o d", o=1))
-        nc.sync.dma_start(out=const_rows[0:1, GAIN_COL:CONST_COLS], in_=ssmax_scale.rearrange("a h b c -> a (h b c)"))
-        ones = keep.tile([P, P], BF16, name="ones")
-        nc.vector.memset(ones[:], 1.0)
-        const_ps = psum_c.tile([P, CONST_COLS], F32, name="const_ps")
-        nc.tensor.matmul(const_ps[:], lhsT=ones[:], rhs=const_rows[:], start=True, stop=True)
-        w_ps = const_ps[:, 0:GAIN_COL].rearrange("p (k d) -> p k d", k=2)
-        gain_ps = const_ps[:, GAIN_COL:CONST_COLS]
+        load_cos_sin(slice(2 * CHUNK, POS_PER_PART))
+        for n in range(1, X_BUFS):
+            load_x(n)
 
-        cos_sin = keep.tile([P, POS_PER_PART, 2, HEAD_DIM], BF16, name="cos_sin")
-        table = keep.tile([P, POS_PER_PART, 2, 2, HEAD_DIM], F32, name="table")
-
-        def load_cos_sin(js):
-            nc.sync.dma_start(out=cos_sin[:, js, 0, :], in_=cos_view[:, js, :])
-            nc.sync.dma_start(out=cos_sin[:, js, 1, 0:HALF], in_=sin_view[:, js, HALF:HEAD_DIM])
-            nc.sync.dma_start(out=cos_sin[:, js, 1, HALF:HEAD_DIM], in_=sin_view[:, js, 0:HALF])
-
-        load_cos_sin(slice(0, CHUNK))
-        load_x(0)
-
-        w_codes = keep.tile([P, PASSES, OUT_COLS], U32, name="w_codes", align_bytes=64)
-        nc.sync.dma_start(
-            out=w_codes[:, :, 0:Q_COLS].bitcast(I32),
-            in_=wq_words.rearrange("g p n t -> p g (n t)").bitcast(I32),
-        )
-        nc.sync.dma_start(
-            out=w_codes[:, :, Q_COLS:OUT_COLS].bitcast(I32),
-            in_=wk_words.rearrange("g p n t -> p g (n t)").bitcast(I32),
-        )
         ident = keep.tile([P, P], F32, name="ident")
         make_identity(nc, ident[:])
 
         eps_col = keep.tile([P, 1], F32, name="eps_col")
         nc.vector.memset(eps_col[:], EPS)
+        warm = keep.tile([P, 1], F32, name="warm")
+        nc.scalar.activation(out=warm[:], in_=eps_col[:], func=ACT.Abs_reciprocal_sqrt)
+
+        table = keep.tile([P, POS_PER_PART, 2, 2, HEAD_DIM], F32, name="table")
 
         def negate_sin(js):
-            nc.vector.tensor_scalar_mul(
-                out=cos_sin[:, js, 1, HALF:HEAD_DIM], in0=cos_sin[:, js, 1, HALF:HEAD_DIM], scalar1=-1.0
-            )
+            nc.vector.tensor_scalar_mul(out=sin_t[:, js, 0:HALF], in0=sin_t[:, js, 0:HALF], scalar1=-1.0)
 
-        def build_table(j):
+        def build_cos(c):
+            js = slice(c * CHUNK, (c + 1) * CHUNK)
             nc.vector.tensor_tensor(
-                out=table[:, j],
-                in0=cos_sin[:, j].unsqueeze(2).to_broadcast([P, 2, 2, HEAD_DIM]),
-                in1=w_ps.unsqueeze(1).to_broadcast([P, 2, 2, HEAD_DIM]),
+                out=table[:, js, 0],
+                in0=cos_t[:, js, :].unsqueeze(2).to_broadcast([P, CHUNK, 2, HEAD_DIM]),
+                in1=w_ps.unsqueeze(1).to_broadcast([P, CHUNK, 2, HEAD_DIM]),
                 op=ALU.mult,
             )
 
-        load_x(1)
-        load_x(2)
-        load_cos_sin(slice(CHUNK, 2 * CHUNK))
-        load_x(3)
-        load_x(4)
-        load_cos_sin(slice(2 * CHUNK, POS_PER_PART))
-        for n in range(5, X_BUFS):
-            load_x(n)
-
-        negate_sin(slice(0, CHUNK))
-        for j in range(CHUNK):
-            build_table(j)
-
-        def table_work(n):
-            if n == -2:
-                negate_sin(slice(CHUNK, 2 * CHUNK))
-            if n in (-2, -1):
-                build_table(CHUNK + 2 * (n + 2))
-                build_table(CHUNK + 2 * (n + 2) + 1)
-            if n == -1:
-                negate_sin(slice(2 * CHUNK, POS_PER_PART))
-            if n >= 0 and n % 2 == 0 and n // 2 + 2 * CHUNK < POS_PER_PART:
-                build_table(n // 2 + 2 * CHUNK)
+        def build_sin(c, kind):
+            js = slice(c * CHUNK, (c + 1) * CHUNK)
+            nc.vector.tensor_tensor(
+                out=table[:, js, 1, kind, :].rearrange("p j (a d) -> p j a d", a=2),
+                in0=sin_t[:, js, :].rearrange("p j (a d) -> p j a d", a=2),
+                in1=w_ps[:, kind, :]
+                .rearrange("p (a d) -> p a d", a=2)[:, ::-1, :]
+                .unsqueeze(1)
+                .to_broadcast([P, CHUNK, 2, HALF]),
+                op=ALU.mult,
+            )
 
         def transpose_unit(n):
             for t in range(UNIT):
@@ -295,7 +291,7 @@ def tile_biboattention_pa_t_kernel(
                     out=partner_term[:, h, t, :].rearrange("p (a d) -> p a d", a=2),
                     in0=acc[:, base : base + HEAD_DIM].rearrange("p (a d) -> p a d", a=2)[:, ::-1, :],
                     scalar=factor,
-                    in1=table[:, j + t, 1, kind, :].rearrange("p (a d) -> p a d", a=2)[:, ::-1, :],
+                    in1=table[:, j + t, 1, kind, :].rearrange("p (a d) -> p a d", a=2),
                     op0=ALU.mult,
                     op1=ALU.mult,
                 )
@@ -323,27 +319,47 @@ def tile_biboattention_pa_t_kernel(
             nc.sync.dma_start(out=q_view[b][:, :, js, :], in_=res[:, 0:Q_HEADS, first : first + count, :])
             nc.sync.dma_start(out=k_view[b, 0][:, js, :], in_=res[:, Q_HEADS, first : first + count, :])
 
-        for n in range(-4, 0):
-            if n + 2 >= 0:
-                quantise_unit(n + 2)
-                project_unit(n + 2)
-            if n + 3 >= 0:
-                regroup_unit(n + 3)
-            transpose_unit(n + 4)
-            load_x(n + 4 + X_BUFS)
-            if n + 2 >= 0:
-                root_mean_square_unit(n + 2)
-            table_work(n)
-        for n in range(UNITS):
+        negate_sin(slice(0, 2 * CHUNK))
+        for c in range(2):
+            build_cos(c)
+            build_sin(c, 0)
+            build_sin(c, 1)
+        transpose_unit(0)
+        load_x(X_BUFS)
+        regroup_unit(0)
+        quantise_unit(0)
+        project_unit(0)
+        root_mean_square_unit(0)
+        transpose_unit(1)
+        load_x(1 + X_BUFS)
+        regroup_unit(1)
+        negate_sin(slice(2 * CHUNK, POS_PER_PART))
+        build_cos(2)
+        build_sin(2, 0)
+        for n in (2, 3):
+            transpose_unit(n)
+            load_x(n + X_BUFS)
+            regroup_unit(n)
+        row_scale_unit(0)
+        build_sin(2, 1)
+        for t in range(UNIT):
+            rotary_tile(0, t)
+        quantise_unit(1)
+        project_unit(1)
+        root_mean_square_unit(1)
+        quantise_unit(2)
+        build_cos(3)
+        build_sin(3, 0)
+        build_sin(3, 1)
+        transpose_unit(4)
+        load_x(4 + X_BUFS)
+        for n in range(1, UNITS):
             for t in range(UNIT):
                 if t == 0:
                     row_scale_unit(n)
-                if n + 2 < UNITS and t == 0:
-                    quantise_unit(n + 2)
-                if t == 1:
-                    table_work(n)
-                if t == 0:
-                    if 1 <= n < UNITS - 1:
+                    if n + 2 < UNITS:
+                        quantise_unit(n + 2)
+                    if n < UNITS - 1:
                         project_unit(n + 1)
                     if n + 3 < UNITS:
                         regroup_unit(n + 3)
@@ -351,7 +367,7 @@ def tile_biboattention_pa_t_kernel(
                         transpose_unit(n + 4)
                         if n + 4 + X_BUFS < UNITS:
                             load_x(n + 4 + X_BUFS)
-                    if 1 <= n < UNITS - 1:
+                    if n < UNITS - 1:
                         root_mean_square_unit(n + 1)
                 rotary_tile(n, t)
                 if n == UNITS - 1:

@@ -176,11 +176,8 @@ def tile_biboattention_pa_t_kernel(
             js = slice(c * CHUNK, (c + 1) * CHUNK)
             nc.vector.tensor_tensor(
                 out=table[:, js, 1, kind, :].rearrange("p j (a d) -> p j a d", a=2),
-                in0=sin_t[:, js, :].rearrange("p j (a d) -> p j a d", a=2),
-                in1=w_ps[:, kind, :]
-                .rearrange("p (a d) -> p a d", a=2)[:, ::-1, :]
-                .unsqueeze(1)
-                .to_broadcast([P, CHUNK, 2, HALF]),
+                in0=sin_t[:, js, :].rearrange("p j (a d) -> p j a d", a=2)[:, :, ::-1, :],
+                in1=w_ps[:, kind, :].rearrange("p (a d) -> p a d", a=2).unsqueeze(1).to_broadcast([P, CHUNK, 2, HALF]),
                 op=ALU.mult,
             )
 
@@ -269,10 +266,9 @@ def tile_biboattention_pa_t_kernel(
                 res = res_pool.tile([P, HEADS, CHUNK, HEAD_DIM], F32, name="res")
                 res_tiles[group] = res
             if t == 0:
-                own_term = work.tile([P, HEADS, UNIT, HEAD_DIM], F32, name="own_term")
-                partner_term = work.tile([P, HEADS, UNIT, HEAD_DIM], F32, name="partner_term")
-                term_tiles[n] = (own_term, partner_term)
-            own_term, partner_term = term_tiles[n]
+                terms = work.tile([P, HEADS, 2 * UNIT, HEAD_DIM], F32, name="terms")
+                term_tiles[n] = terms
+            terms = term_tiles[n]
             row_scale = scale_tiles[n]
             acc = acc_tiles[(n, t)]
             for h in range(HEADS):
@@ -280,35 +276,29 @@ def tile_biboattention_pa_t_kernel(
                 base = h * HEAD_DIM
                 factor = row_scale[:, h, t : t + 1] if h < Q_HEADS else rms_tiles[n][:, h, t : t + 1]
                 nc.vector.scalar_tensor_tensor(
-                    out=own_term[:, h, t, :],
-                    in0=acc[:, base : base + HEAD_DIM],
+                    out=terms[:, h, t : 2 * UNIT - t : 2 * UNIT - 1 - 2 * t, :],
+                    in0=acc[:, base : base + HEAD_DIM].unsqueeze(1).to_broadcast([P, 2, HEAD_DIM]),
                     scalar=factor,
-                    in1=table[:, j + t, 0, kind, :],
-                    op0=ALU.mult,
-                    op1=ALU.mult,
-                )
-                nc.vector.scalar_tensor_tensor(
-                    out=partner_term[:, h, t, :].rearrange("p (a d) -> p a d", a=2),
-                    in0=acc[:, base : base + HEAD_DIM].rearrange("p (a d) -> p a d", a=2)[:, ::-1, :],
-                    scalar=factor,
-                    in1=table[:, j + t, 1, kind, :].rearrange("p (a d) -> p a d", a=2),
+                    in1=table[:, j + t, :, kind, :],
                     op0=ALU.mult,
                     op1=ALU.mult,
                 )
             if n < UNITS - 1:
                 if t == UNIT - 1:
                     nc.gpsimd.tensor_tensor(
-                        out=res_tiles[group][:, :, part * UNIT : (part + 1) * UNIT, :],
-                        in0=own_term[:],
-                        in1=partner_term[:],
+                        out=res_tiles[group][:, :, part * UNIT : (part + 1) * UNIT, :].rearrange(
+                            "p h t (a i) -> p h (t a) i", a=2
+                        ),
+                        in0=terms[:, :, 0:UNIT, :].rearrange("p h t (a i) -> p h (t a) i", a=2),
+                        in1=terms[:, :, UNIT : 2 * UNIT, :].rearrange("p h t (a i) -> p h (t a) i", a=2)[:, :, ::-1, :],
                         op=ALU.add,
                     )
             else:
                 adder = nc.vector if t == UNIT - 1 else nc.gpsimd
                 adder.tensor_tensor(
-                    out=res_tiles[group][:, :, part * UNIT + t, :],
-                    in0=own_term[:, :, t, :],
-                    in1=partner_term[:, :, t, :],
+                    out=res_tiles[group][:, :, part * UNIT + t, :].rearrange("p h (a i) -> p h a i", a=2),
+                    in0=terms[:, :, t, :].rearrange("p h (a i) -> p h a i", a=2),
+                    in1=terms[:, :, 2 * UNIT - 1 - t, :].rearrange("p h (a i) -> p h a i", a=2)[:, :, ::-1, :],
                     op=ALU.add,
                 )
 

@@ -271,7 +271,7 @@ def tile_biboattention_pa_t_kernel(
             terms = term_tiles[n]
             row_scale = scale_tiles[n]
             acc = acc_tiles[(n, t)]
-            for h in range(HEADS):
+            for h in (Q_HEADS, 0, 1):
                 kind = 0 if h < Q_HEADS else 1
                 base = h * HEAD_DIM
                 factor = row_scale[:, h, t : t + 1] if h < Q_HEADS else rms_tiles[n][:, h, t : t + 1]
@@ -346,9 +346,9 @@ def tile_biboattention_pa_t_kernel(
         for n in range(1, UNITS):
             for t in range(UNIT):
                 if t == 0:
-                    row_scale_unit(n)
                     if n + 2 < UNITS:
                         quantise_unit(n + 2)
+                    row_scale_unit(n)
                     if n < UNITS - 1:
                         project_unit(n + 1)
                     if n + 3 < UNITS:

@@ -146,8 +146,9 @@ def tile_biboattention_pa_t_kernel(
                 in_=wk_scales[:, rows, :].rearrange("g r n -> r g n").bitcast(I32),
             )
 
+        load_x(1)
         load_cos_sin(slice(2 * CHUNK, POS_PER_PART))
-        for n in range(1, X_BUFS):
+        for n in range(2, X_BUFS):
             load_x(n)
 
         ident = keep.tile([P, P], F32, name="ident")
@@ -171,6 +172,25 @@ def tile_biboattention_pa_t_kernel(
                 in1=w_ps.unsqueeze(1).to_broadcast([P, CHUNK, 2, HEAD_DIM]),
                 op=ALU.mult,
             )
+
+        def build_position(j, part):
+            if part == 0:
+                nc.vector.tensor_tensor(
+                    out=table[:, j, 0],
+                    in0=cos_t[:, j, :].unsqueeze(1).to_broadcast([P, 2, HEAD_DIM]),
+                    in1=w_ps,
+                    op=ALU.mult,
+                )
+            else:
+                nc.vector.tensor_tensor(
+                    out=table[:, j, 1].rearrange("p k (a d) -> p k a d", a=2),
+                    in0=sin_t[:, j, :]
+                    .rearrange("p (a d) -> p a d", a=2)[:, ::-1, :]
+                    .unsqueeze(1)
+                    .to_broadcast([P, 2, 2, HALF]),
+                    in1=w_ps.rearrange("p k (a d) -> p k a d", a=2),
+                    op=ALU.mult,
+                )
 
         def build_sin(c, kind):
             js = slice(c * CHUNK, (c + 1) * CHUNK)
@@ -317,37 +337,38 @@ def tile_biboattention_pa_t_kernel(
         transpose_unit(0)
         load_x(X_BUFS)
         regroup_unit(0)
-        quantise_unit(0)
-        project_unit(0)
-        root_mean_square_unit(0)
         transpose_unit(1)
         load_x(1 + X_BUFS)
+        quantise_unit(0)
+        project_unit(0)
         regroup_unit(1)
+        root_mean_square_unit(0)
         negate_sin(slice(2 * CHUNK, POS_PER_PART))
         build_cos(2)
         build_sin(2, 0)
-        for n in (2, 3):
-            transpose_unit(n)
-            load_x(n + X_BUFS)
-            regroup_unit(n)
-        row_scale_unit(0)
         build_sin(2, 1)
-        for t in range(UNIT):
-            rotary_tile(0, t)
+        transpose_unit(2)
+        load_x(2 + X_BUFS)
         quantise_unit(1)
         project_unit(1)
+        regroup_unit(2)
+        row_scale_unit(0)
+        for t in range(UNIT):
+            rotary_tile(0, t)
         root_mean_square_unit(1)
+        for n in (3, 4):
+            transpose_unit(n)
+            load_x(n + X_BUFS)
+            if n == 3:
+                regroup_unit(n)
         quantise_unit(2)
-        build_cos(3)
-        build_sin(3, 0)
-        build_sin(3, 1)
-        transpose_unit(4)
-        load_x(4 + X_BUFS)
         for n in range(1, UNITS):
             for t in range(UNIT):
                 if t == 0:
                     if n + 2 < UNITS:
                         quantise_unit(n + 2)
+                    if 2 <= n < 2 + 2 * CHUNK:
+                        build_position(3 * CHUNK + (n - 2) // 2, (n - 2) % 2)
                     row_scale_unit(n)
                     if n < UNITS - 1:
                         project_unit(n + 1)

@@ -102,17 +102,21 @@ def tile_biboattention_pa_t_kernel(
         cos_t = keep.tile([P, POS_PER_PART, HEAD_DIM], BF16, name="cos_t")
         sin_t = keep.tile([P, POS_PER_PART, HEAD_DIM], BF16, name="sin_t")
 
-        def load_cos_sin(js):
+        def load_cos(js):
             nc.sync.dma_start(out=cos_t[:, js, :], in_=cos_view[:, js, :])
+
+        def load_sin(js):
             nc.sync.dma_start(out=sin_t[:, js, :], in_=sin_view[:, js, :])
 
-        load_cos_sin(slice(0, 2 * CHUNK))
+        load_cos(slice(0, 2 * CHUNK))
 
         const_rows = keep.tile([P, CONST_COLS], BF16, name="const_rows")
         nc.gpsimd.memset(const_rows[:], 0.0)
         nc.sync.dma_start(out=const_rows[0:1, 0:HEAD_DIM], in_=q_norm_w.rearrange("(o d) -> o d", o=1))
         nc.sync.dma_start(out=const_rows[0:1, HEAD_DIM:GAIN_COL], in_=k_norm_w.rearrange("(o d) -> o d", o=1))
         nc.sync.dma_start(out=const_rows[0:1, GAIN_COL:CONST_COLS], in_=ssmax_scale.rearrange("a h b c -> a (h b c)"))
+        load_sin(slice(0, 2 * CHUNK))
+
         ones = keep.tile([P, P], BF16, name="ones")
         nc.vector.memset(ones[:], 1.0)
         const_ps = psum_c.tile([P, CONST_COLS], F32, name="const_ps")
@@ -147,7 +151,8 @@ def tile_biboattention_pa_t_kernel(
             )
 
         load_x(1)
-        load_cos_sin(slice(2 * CHUNK, POS_PER_PART))
+        load_cos(slice(2 * CHUNK, POS_PER_PART))
+        load_sin(slice(2 * CHUNK, POS_PER_PART))
         for n in range(2, X_BUFS):
             load_x(n)
 
@@ -313,14 +318,15 @@ def tile_biboattention_pa_t_kernel(
                         in1=terms[:, :, UNIT : 2 * UNIT, :].rearrange("p h t (a i) -> p h (t a) i", a=2)[:, :, ::-1, :],
                         op=ALU.add,
                     )
-            else:
-                adder = nc.vector if t == UNIT - 1 else nc.gpsimd
-                adder.tensor_tensor(
-                    out=res_tiles[group][:, :, part * UNIT + t, :].rearrange("p h (a i) -> p h a i", a=2),
-                    in0=terms[:, :, t, :].rearrange("p h (a i) -> p h a i", a=2),
-                    in1=terms[:, :, 2 * UNIT - 1 - t, :].rearrange("p h (a i) -> p h a i", a=2)[:, :, ::-1, :],
-                    op=ALU.add,
-                )
+            elif t == UNIT - 1:
+                for s in range(UNIT):
+                    nc.vector.tensor_tensor(
+                        out=res_tiles[group][:, :, part * UNIT + s, :].rearrange("p h (a i) -> p h a i", a=2),
+                        in0=terms[:, :, s, :].rearrange("p h (a i) -> p h a i", a=2),
+                        in1=terms[:, :, 2 * UNIT - 1 - s, :].rearrange("p h (a i) -> p h a i", a=2)[:, :, ::-1, :],
+                        op=ALU.add,
+                    )
+                    store(GROUPS - 1, CHUNK - UNIT + s, 1)
 
         def store(group, first, count):
             c, b = divmod(group, BATCH)
@@ -347,20 +353,18 @@ def tile_biboattention_pa_t_kernel(
         build_cos(2)
         build_sin(2, 0)
         build_sin(2, 1)
-        transpose_unit(2)
-        load_x(2 + X_BUFS)
+        for n in (2, 3):
+            transpose_unit(n)
+            load_x(n + X_BUFS)
+            regroup_unit(n)
         quantise_unit(1)
         project_unit(1)
-        regroup_unit(2)
         row_scale_unit(0)
         for t in range(UNIT):
             rotary_tile(0, t)
         root_mean_square_unit(1)
-        for n in (3, 4):
-            transpose_unit(n)
-            load_x(n + X_BUFS)
-            if n == 3:
-                regroup_unit(n)
+        transpose_unit(4)
+        load_x(4 + X_BUFS)
         quantise_unit(2)
         for n in range(1, UNITS):
             for t in range(UNIT):
@@ -381,8 +385,6 @@ def tile_biboattention_pa_t_kernel(
                     if n < UNITS - 1:
                         root_mean_square_unit(n + 1)
                 rotary_tile(n, t)
-                if n == UNITS - 1:
-                    store(GROUPS - 1, CHUNK - UNIT + t, 1)
             group, part = divmod(n, UNITS_PER_GROUP)
             if n == UNITS - 2:
                 store(group, 0, UNIT)

import math
from contextlib import ExitStack

import concourse.mybir as mybir
from concourse.masks import make_identity

F32 = mybir.dt.float32
BF16 = mybir.dt.bfloat16
I32 = mybir.dt.int32
U32 = mybir.dt.uint32
U8 = mybir.dt.uint8
FP8X4 = mybir.dt.float8_e4m3fn_x4
ALU = mybir.AluOpType
ACT = mybir.ActivationFunctionType

P = 128
BATCH = 4
SEQ = 2048
HIDDEN = 1024
HEAD_DIM = 128
HALF = HEAD_DIM // 2
Q_HEADS = 2
HEADS = Q_HEADS + 1
Q_COLS = Q_HEADS * HEAD_DIM
OUT_COLS = HEADS * HEAD_DIM
EPS = 1e-6

K_PASS = 512
PASSES = HIDDEN // K_PASS
WORDS_PER_PASS = K_PASS // 2

POS_PER_PART = SEQ // P
CHUNK = 4
CHUNKS = POS_PER_PART // CHUNK
GROUPS = CHUNKS * BATCH
UNIT = 2
UNITS_PER_GROUP = CHUNK // UNIT
UNITS = GROUPS * UNITS_PER_GROUP
X_BUFS = 8
GAIN_COL = 2 * HEAD_DIM
CONST_COLS = GAIN_COL + Q_HEADS

FLOPS = 2 * BATCH * SEQ * HIDDEN * OUT_COLS


def tile_biboattention_pa_t_kernel(
    tc,
    hidden_states,
    cos,
    sin,
    wq_words,
    wq_scales,
    wk_words,
    wk_scales,
    q_norm_w,
    k_norm_w,
    ssmax_scale,
    out_0,
    out_1,
):
    nc = tc.nc

    x_view = hidden_states.rearrange("b (p j) k -> b p j k", j=POS_PER_PART)
    cos_view = cos.rearrange("(p j) d -> p j d", j=POS_PER_PART)
    sin_view = sin.rearrange("(p j) d -> p j d", j=POS_PER_PART)
    q_view = out_0.rearrange("b h (p j) d -> b p h j d", j=POS_PER_PART)
    k_view = out_1.rearrange("b h (p j) d -> b h p j d", j=POS_PER_PART)

    with ExitStack() as ctx:
        keep = ctx.enter_context(tc.tile_pool(name="keep", bufs=1))
        x_pool = ctx.enter_context(tc.tile_pool(name="x", bufs=X_BUFS))
        mx_pool = ctx.enter_context(tc.tile_pool(name="mx", bufs=3))
        row_pool = ctx.enter_context(tc.tile_pool(name="row", bufs=3))
        work = ctx.enter_context(tc.tile_pool(name="work", bufs=3))
        res_pool = ctx.enter_context(tc.tile_pool(name="res", bufs=3))
        psum_c = ctx.enter_context(tc.psum_pool(name="psum_c", bufs=1))
        psum_t = ctx.enter_context(tc.psum_pool(name="psum_t", bufs=3))
        psum_o = ctx.enter_context(tc.psum_pool(name="psum_o", bufs=2 * UNIT))
        ctx.enter_context(tc.manual_schedule())

        x_tiles = {}
        xt_tiles = {}
        grouped_tiles = {}
        code_tiles = {}
        acc_tiles = {}
        rms_tiles = {}
        scale_tiles = {}
        res_tiles = {}
        term_tiles = {}

        def first_position(n):
            group, part = divmod(n, UNITS_PER_GROUP)
            c, b = divmod(group, BATCH)
            return b, c * CHUNK + part * UNIT

        def load_x(n):
            b, j = first_position(n)
            x_sb = x_pool.tile([P, UNIT, HIDDEN], BF16, name="x_sb")
            nc.sync.dma_start(out=x_sb[:], in_=x_view[b][:, j : j + UNIT, :])
            x_tiles[n] = x_sb

        cos_t = keep.tile([P, POS_PER_PART, HEAD_DIM], BF16, name="cos_t")
        sin_t = keep.tile([P, POS_PER_PART, HEAD_DIM], BF16, name="sin_t")

        def load_cos(js):
            nc.sync.dma_start(out=cos_t[:, js, :], in_=cos_view[:, js, :])

        def load_sin(js):
            nc.sync.dma_start(out=sin_t[:, js, :], in_=sin_view[:, js, :])

        load_cos(slice(0, 2 * CHUNK))

        const_rows = keep.tile([P, CONST_COLS], BF16, name="const_rows")
        nc.gpsimd.memset(const_rows[:], 0.0)
        nc.sync.dma_start(out=const_rows[0:1, 0:HEAD_DIM], in_=q_norm_w.rearrange("(o d) -> o d", o=1))
        nc.sync.dma_start(out=const_rows[0:1, HEAD_DIM:GAIN_COL], in_=k_norm_w.rearrange("(o d) -> o d", o=1))
        nc.sync.dma_start(out=const_rows[0:1, GAIN_COL:CONST_COLS], in_=ssmax_scale.rearrange("a h b c -> a (h b c)"))
        load_sin(slice(0, 2 * CHUNK))

        ones = keep.tile([P, P], BF16, name="ones")
        nc.vector.memset(ones[:], 1.0)
        const_ps = psum_c.tile([P, CONST_COLS], F32, name="const_ps")
        nc.tensor.matmul(const_ps[:], lhsT=ones[:], rhs=const_rows[:], start=True, stop=True)
        w_ps = const_ps[:, 0:GAIN_COL].rearrange("p (k d) -> p k d", k=2)
        gain_ps = const_ps[:, GAIN_COL:CONST_COLS]

        load_x(0)

        w_codes = keep.tile([P, PASSES, OUT_COLS], U32, name="w_codes", align_bytes=64)
        nc.sync.dma_start(
            out=w_codes[:, :, 0:Q_COLS].bitcast(I32),
            in_=wq_words.rearrange("g p n t -> p g (n t)").bitcast(I32),
        )
        nc.sync.dma_start(
            out=w_codes[:, :, Q_COLS:OUT_COLS].bitcast(I32),
            in_=wk_words.rearrange("g p n t -> p g (n t)").bitcast(I32),
        )

        w_scales = keep.tile([P, PASSES, OUT_COLS], U8, name="w_scales", align_bytes=64)
        nc.vector.memset(w_scales[:].bitcast(I32), 0)
        for quad in range(4):
            rows = slice(4 * quad, 4 * quad + 4)
            parts = slice(32 * quad, 32 * quad + 4)
            nc.sync.dma_start(
                out=w_scales[parts, :, 0:Q_COLS].bitcast(I32),
                in_=wq_scales[:, rows, :].rearrange("g r n -> r g n").bitcast(I32),
            )
            nc.sync.dma_start(
                out=w_scales[parts, :, Q_COLS:OUT_COLS].bitcast(I32),
                in_=wk_scales[:, rows, :].rearrange("g r n -> r g n").bitcast(I32),
            )

        load_x(1)
        load_cos(slice(2 * CHUNK, POS_PER_PART))
        load_sin(slice(2 * CHUNK, POS_PER_PART))
        for n in range(2, X_BUFS):
            load_x(n)

        ident = keep.tile([P, P], F32, name="ident")
        make_identity(nc, ident[:])

        eps_col = keep.tile([P, 1], F32, name="eps_col")
        nc.vector.memset(eps_col[:], EPS)
        warm = keep.tile([P, 1], F32, name="warm")
        nc.scalar.activation(out=warm[:], in_=eps_col[:], func=ACT.Abs_reciprocal_sqrt)

        table = keep.tile([P, POS_PER_PART, 2, 2, HEAD_DIM], F32, name="table")

        def negate_sin(js):
            nc.vector.tensor_scalar_mul(out=sin_t[:, js, 0:HALF], in0=sin_t[:, js, 0:HALF], scalar1=-1.0)

        def build_cos(c):
            js = slice(c * CHUNK, (c + 1) * CHUNK)
            nc.vector.tensor_tensor(
                out=table[:, js, 0],
                in0=cos_t[:, js, :].unsqueeze(2).to_broadcast([P, CHUNK, 2, HEAD_DIM]),
                in1=w_ps.unsqueeze(1).to_broadcast([P, CHUNK, 2, HEAD_DIM]),
                op=ALU.mult,
            )

        def build_position(j, part):
            if part == 0:
                nc.vector.tensor_tensor(
                    out=table[:, j, 0],
                    in0=cos_t[:, j, :].unsqueeze(1).to_broadcast([P, 2, HEAD_DIM]),
                    in1=w_ps,
                    op=ALU.mult,
                )
            else:
                nc.vector.tensor_tensor(
                    out=table[:, j, 1].rearrange("p k (a d) -> p k a d", a=2),
                    in0=sin_t[:, j, :]
                    .rearrange("p (a d) -> p a d", a=2)[:, ::-1, :]
                    .unsqueeze(1)
                    .to_broadcast([P, 2, 2, HALF]),
                    in1=w_ps.rearrange("p k (a d) -> p k a d", a=2),
                    op=ALU.mult,
                )

        def build_sin(c, kind):
            js = slice(c * CHUNK, (c + 1) * CHUNK)
            nc.vector.tensor_tensor(
                out=table[:, js, 1, kind, :].rearrange("p j (a d) -> p j a d", a=2),
                in0=sin_t[:, js, :].rearrange("p j (a d) -> p j a d", a=2)[:, :, ::-1, :],
                in1=w_ps[:, kind, :].rearrange("p (a d) -> p a d", a=2).unsqueeze(1).to_broadcast([P, CHUNK, 2, HALF]),
                op=ALU.mult,
            )

        def transpose_unit(n):
            for t in range(UNIT):
                words = x_tiles[n][:, t, :].bitcast(F32)
                xt = psum_t.tile([P, PASSES * 2, P], F32, name="xt")
                for g in range(PASSES):
                    for u in range(2):
                        first = WORDS_PER_PASS * g + u
                        nc.tensor.transpose(
                            xt[:, 2 * g + u, :], words[:, first : WORDS_PER_PASS * (g + 1) : 2], ident[:]
                        )
                xt_tiles[(n, t)] = xt

        def regroup_unit(n):
            grouped = mx_pool.tile([P, UNIT, HIDDEN], BF16, name="grouped", align_bytes=64)
            for t in range(UNIT):
                nc.scalar.copy(
                    out=grouped[:, t, :].bitcast(F32).rearrange("p (g r u) -> p g r u", g=PASSES, u=2),
                    in_=xt_tiles[(n, t)][:].rearrange("p (g u) r -> p g r u", u=2),
                )
            grouped_tiles[n] = grouped

        def quantise_unit(n):
            x_codes = mx_pool.tile([P, UNIT * PASSES * P], U32, name="x_codes", align_bytes=64)
            x_scales = mx_pool.tile([P, UNIT * PASSES * P], U8, name="x_scales", align_bytes=64)
            code_tiles[n] = (x_codes, x_scales)
            nc.vector.quantize_mx(
                out=x_codes[:].bitcast(FP8X4),
                scales=x_scales[:],
                in_=grouped_tiles[n][:].rearrange("p t k -> p (t k)"),
            )

        def project_unit(n):
            x_codes, x_scales = code_tiles[n]
            for t in range(UNIT):
                acc = psum_o.tile([P, OUT_COLS], F32, name="acc")
                for lo, hi in ((0, Q_COLS), (Q_COLS, OUT_COLS)):
                    for g in range(PASSES):
                        tokens = slice((t * PASSES + g) * P, (t * PASSES + g + 1) * P)
                        nc.tensor.matmul_mx(
                            out=acc[:, lo:hi],
                            lhsT=x_codes[:, tokens].bitcast(FP8X4),
                            lhsT_scale=x_scales[:, tokens],
                            rhs=w_codes[:, g, lo:hi].bitcast(FP8X4),
                            rhs_scale=w_scales[:, g, lo:hi],
                            start=(g == 0),
                            stop=(g == PASSES - 1),
                        )
                acc_tiles[(n, t)] = acc

        def root_mean_square_unit(n):
            sumsq = row_pool.tile([P, HEADS, UNIT], F32, name="sumsq")
            squares = work.tile([P, HEADS, UNIT, HEAD_DIM], BF16, name="squares")
            for t in range(UNIT):
                for h in range(HEADS):
                    nc.scalar.activation(
                        out=squares[:, h, t, :],
                        in_=acc_tiles[(n, t)][:, h * HEAD_DIM : (h + 1) * HEAD_DIM],
                        func=ACT.Square,
                        accum_out=sumsq[:, h, t : t + 1],
                    )
            rms = row_pool.tile([P, HEADS, UNIT], F32, name="rms")
            nc.scalar.activation(
                out=rms[:], in_=sumsq[:], func=ACT.Abs_reciprocal_sqrt, scale=1.0 / HEAD_DIM, bias=eps_col[:, 0:1]
            )
            rms_tiles[n] = rms

        def row_scale_unit(n):
            row_scale = row_pool.tile([P, Q_HEADS, UNIT], F32, name="row_scale")
            nc.vector.scalar_tensor_tensor(
                out=row_scale[:],
                in0=rms_tiles[n][:, 0:Q_HEADS, :],
                scalar=math.log(SEQ),
                in1=gain_ps.unsqueeze(2).to_broadcast([P, Q_HEADS, UNIT]),
                op0=ALU.mult,
                op1=ALU.mult,
            )
            scale_tiles[n] = row_scale

        def rotary_tile(n, t):
            group, part = divmod(n, UNITS_PER_GROUP)
            b, j = first_position(n)
            if part == 0 and t == 0:
                res = res_pool.tile([P, HEADS, CHUNK, HEAD_DIM], F32, name="res")
                res_tiles[group] = res
            if t == 0:
                terms = work.tile([P, HEADS, 2 * UNIT, HEAD_DIM], F32, name="terms")
                term_tiles[n] = terms
            terms = term_tiles[n]
            row_scale = scale_tiles[n]
            acc = acc_tiles[(n, t)]
            for h in (Q_HEADS, 0, 1):
                kind = 0 if h < Q_HEADS else 1
                base = h * HEAD_DIM
                factor = row_scale[:, h, t : t + 1] if h < Q_HEADS else rms_tiles[n][:, h, t : t + 1]
                nc.vector.scalar_tensor_tensor(
                    out=terms[:, h, t : 2 * UNIT - t : 2 * UNIT - 1 - 2 * t, :],
                    in0=acc[:, base : base + HEAD_DIM].unsqueeze(1).to_broadcast([P, 2, HEAD_DIM]),
                    scalar=factor,
                    in1=table[:, j + t, :, kind, :],
                    op0=ALU.mult,
                    op1=ALU.mult,
                )
            if n < UNITS - 1:
                if t == UNIT - 1:
                    nc.gpsimd.tensor_tensor(
                        out=res_tiles[group][:, :, part * UNIT : (part + 1) * UNIT, :].rearrange(
                            "p h t (a i) -> p h (t a) i", a=2
                        ),
                        in0=terms[:, :, 0:UNIT, :].rearrange("p h t (a i) -> p h (t a) i", a=2),
                        in1=terms[:, :, UNIT : 2 * UNIT, :].rearrange("p h t (a i) -> p h (t a) i", a=2)[:, :, ::-1, :],
                        op=ALU.add,
                    )
            elif t == UNIT - 1:
                for s in range(UNIT):
                    nc.vector.tensor_tensor(
                        out=res_tiles[group][:, :, part * UNIT + s, :].rearrange("p h (a i) -> p h a i", a=2),
                        in0=terms[:, :, s, :].rearrange("p h (a i) -> p h a i", a=2),
                        in1=terms[:, :, 2 * UNIT - 1 - s, :].rearrange("p h (a i) -> p h a i", a=2)[:, :, ::-1, :],
                        op=ALU.add,
                    )
                    store(GROUPS - 1, CHUNK - UNIT + s, 1)

        def store(group, first, count):
            c, b = divmod(group, BATCH)
            js = slice(c * CHUNK + first, c * CHUNK + first + count)
            res = res_tiles[group]
            nc.sync.dma_start(out=q_view[b][:, :, js, :], in_=res[:, 0:Q_HEADS, first : first + count, :])
            nc.sync.dma_start(out=k_view[b, 0][:, js, :], in_=res[:, Q_HEADS, first : first + count, :])

        negate_sin(slice(0, 2 * CHUNK))
        for c in range(2):
            build_cos(c)
            build_sin(c, 0)
            build_sin(c, 1)
        transpose_unit(0)
        load_x(X_BUFS)
        regroup_unit(0)
        transpose_unit(1)
        load_x(1 + X_BUFS)
        quantise_unit(0)
        project_unit(0)
        regroup_unit(1)
        root_mean_square_unit(0)
        negate_sin(slice(2 * CHUNK, POS_PER_PART))
        build_cos(2)
        build_sin(2, 0)
        build_sin(2, 1)
        for n in (2, 3):
            transpose_unit(n)
            load_x(n + X_BUFS)
            regroup_unit(n)
        quantise_unit(1)
        project_unit(1)
        row_scale_unit(0)
        for t in range(UNIT):
            rotary_tile(0, t)
        root_mean_square_unit(1)
        transpose_unit(4)
        load_x(4 + X_BUFS)
        quantise_unit(2)
        for n in range(1, UNITS):
            for t in range(UNIT):
                if t == 0:
                    if n + 2 < UNITS:
                        quantise_unit(n + 2)
                    if 2 <= n < 2 + 2 * CHUNK:
                        build_position(3 * CHUNK + (n - 2) // 2, (n - 2) % 2)
                    row_scale_unit(n)
                    if n < UNITS - 1:
                        project_unit(n + 1)
                    if n + 3 < UNITS:
                        regroup_unit(n + 3)
                    if n + 4 < UNITS:
                        transpose_unit(n + 4)
                        if n + 4 + X_BUFS < UNITS:
                            load_x(n + 4 + X_BUFS)
                    if n < UNITS - 1:
                        root_mean_square_unit(n + 1)
                rotary_tile(n, t)
            group, part = divmod(n, UNITS_PER_GROUP)
            if n == UNITS - 2:
                store(group, 0, UNIT)
            elif group < GROUPS - 1 and part == UNITS_PER_GROUP - 1:
                store(group, 0, CHUNK)
